import numpy as np
import ml_dtypes


def mxq(x, axis, fmt="e4m3"):
    dtype, down = {"e4m3": (ml_dtypes.float8_e4m3fn, 7), "e5m2": (ml_dtypes.float8_e5m2, 14)}[fmt]
    v = np.moveaxis(np.asarray(x, np.float32).astype(ml_dtypes.bfloat16).astype(np.float64), axis, -1)
    blocks = v.reshape(v.shape[:-1] + (-1, 32))
    amax = np.abs(blocks).max(-1, keepdims=True)
    byte = np.maximum(np.where(amax > 0, np.frexp(amax)[1] - 1 + 127, 0) - down, 1)
    scale = np.exp2(byte - 127.0)
    codes = (blocks / scale).astype(np.float32).astype(dtype).astype(np.float64)
    return np.moveaxis((codes * scale).reshape(v.shape), -1, axis)


WIDE = False


def mx_kscale(k):
    if not WIDE:
        return np.ones(k)
    levels = np.array([10, -10, 5, -5, 0])
    if k % 512:
        return np.exp2(np.random.permutation(np.resize(levels, k // 32))).repeat(32)
    a = np.empty((k // 512, 16))
    for p in range(k // 512):
        a[p, :8] = np.random.permutation(np.resize(levels, 8))
        for g in range(8):
            far = levels[np.abs(levels - a[p, g]) >= 10]
            a[p, g + 8] = far[np.random.randint(len(far))]
    return np.exp2(a.ravel()).repeat(32)


BF16 = ml_dtypes.bfloat16


def bf(x):
    return np.asarray(x, np.float32).astype(BF16)


def f64(x):
    return np.asarray(x).astype(np.float64)


S, E, H, DH = 1024, 1024, 16, 64
W = H * DH


def rotate_half(t):
    return np.stack((-t[..., 1::2], t[..., ::2]), axis=-1).reshape(t.shape)


def setup_inputs():
    s = mx_kscale(E)
    return {"hidden_states": bf(np.random.standard_normal((S, E)) * s),
            "cos": bf(np.random.uniform(size=(S, DH))),
            "sin": bf(np.random.uniform(size=(S, DH))),
            "w_qkv": bf(np.random.standard_normal((E, 3 * W)) * 2.0 / np.sqrt(E) / s[:, None]),
            "b_qkv": bf(np.random.standard_normal(3 * W) * 0.3)}


def reference(hidden_states, cos, sin, w_qkv, b_qkv):
    qkv = ((mxq(f64(hidden_states), 1, "e4m3") @ mxq(f64(w_qkv), 0, "e4m3")) + f64(b_qkv)).reshape(S, 3, H, DH)
    q, k, v = qkv[:, 0], qkv[:, 1], qkv[:, 2]
    c = f64(cos)[:, None, :]
    sn = f64(sin)[:, None, :]
    q_rot = q * c + rotate_half(q) * sn
    k_rot = k * c + rotate_half(k) * sn
    return q_rot, k_rot, v

@@ -1,0 +1,320 @@
+from contextlib import ExitStack
+
+import concourse.mybir as mybir
+from concourse.masks import make_identity
+
+F32 = mybir.dt.float32
+BF16 = mybir.dt.bfloat16
+U32 = mybir.dt.uint32
+U8 = mybir.dt.uint8
+FP8X4 = mybir.dt.float8_e4m3fn_x4
+ADD = mybir.AluOpType.add
+MULT = mybir.AluOpType.mult
+
+S, E, HEADS, DH = 1024, 1024, 16, 64
+WIDTH = HEADS * DH
+HALF = DH // 2
+P = 128
+PACK = 4
+K_PASS = P * PACK
+PASSES = E // K_PASS
+S_BLOCKS = S // P
+CHUNK_BLOCKS = 4
+CHUNK = CHUNK_BLOCKS * P
+CHUNKS = S_BLOCKS // CHUNK_BLOCKS
+GROUP = 512
+GROUPS = 3 * WIDTH // GROUP
+ROTATED_GROUPS = 2 * WIDTH // GROUP
+GROUP_TILES = GROUP // P
+TILE_HEADS = P // DH
+PAIR = 2
+
+FLOPS = 2 * S * E * 3 * WIDTH
+
+
+def tile_arlowvisionattention_pa_kernel(
+    tc, hidden_states, cos, sin, w_qkv, b_qkv, out_0, out_1, out_2
+):
+    nc = tc.nc
+    with ExitStack() as ctx:
+        const = ctx.enter_context(tc.tile_pool(name="const", bufs=1))
+        operands = ctx.enter_context(tc.tile_pool(name="operands", bufs=1))
+        work = ctx.enter_context(tc.tile_pool(name="work", bufs=3))
+        psum_mx = ctx.enter_context(tc.psum_pool(name="psum_mx", bufs=5))
+        psum_plain = ctx.enter_context(tc.psum_pool(name="psum_plain", bufs=3))
+
+        x_rows = hidden_states.rearrange("(p b) k -> p b k", b=S_BLOCKS)
+        out_rows = [
+            out.rearrange("(p b) h d -> p b (h d)", b=S_BLOCKS) for out in (out_0, out_1, out_2)
+        ]
+
+        x_raw = [
+            operands.tile([P, CHUNK_BLOCKS, E], BF16, name="x_raw%d" % c) for c in range(CHUNKS)
+        ]
+        x_grouped = [
+            operands.tile([P, PASSES, CHUNK, PACK], BF16, name="x_grouped%d" % c, align_bytes=64)
+            for c in range(CHUNKS)
+        ]
+        x_codes = [
+            operands.tile([P, PASSES, CHUNK], U32, name="x_codes%d" % c, align_bytes=64)
+            for c in range(CHUNKS)
+        ]
+        x_scales = [
+            operands.tile([P, PASSES, CHUNK], U8, name="x_scales%d" % c, align_bytes=64)
+            for c in range(CHUNKS)
+        ]
+        w_raw = [
+            operands.tile([P, PASSES, PACK, GROUP], BF16, name="w_raw%d" % n) for n in range(GROUPS)
+        ]
+        w_codes = [
+            operands.tile([P, PASSES, GROUP], U32, name="w_codes%d" % n, align_bytes=64)
+            for n in range(GROUPS)
+        ]
+        w_scales = [
+            operands.tile([P, PASSES, GROUP], U8, name="w_scales%d" % n, align_bytes=64)
+            for n in range(GROUPS)
+        ]
+
+        cos_raw = const.tile([P, S_BLOCKS, DH], BF16)
+        sin_raw = const.tile([P, S_BLOCKS, DH], BF16)
+        nc.scalar.dma_start(out=cos_raw[:], in_=cos.rearrange("(p b) d -> p b d", b=S_BLOCKS))
+        nc.scalar.dma_start(out=sin_raw[:], in_=sin.rearrange("(p b) d -> p b d", b=S_BLOCKS))
+
+        rotated_tiles = ROTATED_GROUPS * GROUP_TILES
+        bias_rows = const.tile([P, P], BF16)
+        nc.vector.memset(bias_rows[:], 0.0)
+        nc.scalar.dma_start(
+            out=bias_rows[0:rotated_tiles, :],
+            in_=b_qkv[0 : rotated_tiles * P].rearrange("(t n) -> t n", n=P),
+        )
+        v_bias_row = const.tile([P, WIDTH], BF16)
+        nc.vector.memset(v_bias_row[:], 0.0)
+        nc.scalar.dma_start(
+            out=v_bias_row[0:1, :],
+            in_=b_qkv[2 * WIDTH : 3 * WIDTH].rearrange("(o n) -> o n", o=1),
+        )
+
+        def load_weights(n):
+            for g in range(PASSES):
+                nc.sync.dma_start(
+                    out=w_raw[n][:, g, :, :],
+                    in_=w_qkv[
+                        g * K_PASS : (g + 1) * K_PASS, n * GROUP : (n + 1) * GROUP
+                    ].rearrange("(q t) n -> q t n", t=PACK),
+                )
+
+        load_weights(0)
+        for c in range(CHUNKS):
+            nc.sync.dma_start(
+                out=x_raw[c][:], in_=x_rows[:, c * CHUNK_BLOCKS : (c + 1) * CHUNK_BLOCKS, :]
+            )
+        for n in range(1, GROUPS):
+            load_weights(n)
+
+        ident = const.tile([P, P], F32)
+        make_identity(nc, ident[:])
+        swap = const.tile([P, P], F32)
+        swap_pairs = swap[:].rearrange("r (i two) -> r i two", two=2)
+        ident_pairs = ident[:].rearrange("r (i two) -> r i two", two=2)
+        for two in range(2):
+            nc.vector.tensor_copy(out=swap_pairs[:, :, two], in_=ident_pairs[:, :, 1 - two])
+
+        bias_rows_f32 = const.tile([P, P], F32)
+        nc.vector.tensor_copy(out=bias_rows_f32[:], in_=bias_rows[:])
+        bias_flipped = psum_plain.tile([P, P], F32, tag="plain")
+        nc.tensor.transpose(out=bias_flipped[:], in_=bias_rows_f32[:], identity=ident[:])
+        bias_cols = const.tile([P, rotated_tiles], F32)
+        nc.vector.tensor_copy(out=bias_cols[:], in_=bias_flipped[:, 0:rotated_tiles])
+
+        own_factor = const.tile([P, S_BLOCKS, TILE_HEADS, DH], F32)
+        nc.vector.tensor_copy(
+            out=own_factor[:],
+            in_=cos_raw[:].unsqueeze(2).to_broadcast([P, S_BLOCKS, TILE_HEADS, DH]),
+        )
+        sin_pairs = sin_raw[:].rearrange("p b (i two) -> p b i two", two=2)
+        crossed = const.tile([P, S_BLOCKS, HALF, 2], F32)
+        nc.vector.tensor_copy(out=crossed[:, :, :, 0], in_=sin_pairs[:, :, :, 1])
+        nc.vector.tensor_scalar_mul(out=crossed[:, :, :, 1], in0=sin_pairs[:, :, :, 0], scalar1=-1.0)
+        neighbour_factor = const.tile([P, S_BLOCKS, TILE_HEADS, DH], F32)
+        nc.vector.tensor_copy(
+            out=neighbour_factor[:],
+            in_=crossed[:]
+            .rearrange("p b i two -> p b (i two)")
+            .unsqueeze(2)
+            .to_broadcast([P, S_BLOCKS, TILE_HEADS, DH]),
+        )
+
+        def flip_table(table, c):
+            flipped = psum_plain.tile([P, CHUNK_BLOCKS, P], F32, tag="plain")
+            for j in range(CHUNK_BLOCKS):
+                nc.tensor.transpose(
+                    out=flipped[:, j, :],
+                    in_=table[:, c * CHUNK_BLOCKS + j, :, :].rearrange("p h d -> p (h d)"),
+                    identity=ident[:],
+                )
+            return flipped
+
+        cos_t = const.tile([P, CHUNKS, CHUNK], F32)
+        sin_t = const.tile([P, CHUNKS, CHUNK], F32)
+        for c in range(CHUNKS):
+            for table, table_t in ((own_factor, cos_t), (neighbour_factor, sin_t)):
+                nc.scalar.copy(
+                    out=table_t[:, c, :],
+                    in_=flip_table(table, c)[:].rearrange("r j p -> r (j p)"),
+                )
+
+        def quantise_weights(n, g):
+            grouped = work.tile([P, GROUP, PACK], BF16, align_bytes=64, tag="w_grouped")
+            nc.scalar.copy(
+                out=grouped[:].rearrange("q (c i) t -> q c t i", i=4),
+                in_=w_raw[n][:, g, :, :].rearrange("q t (c i) -> q c t i", i=4),
+            )
+            nc.vector.quantize_mx(
+                out=w_codes[n][:, g, :].bitcast(FP8X4),
+                scales=w_scales[n][:, g, :],
+                in_=grouped[:].rearrange("q c t -> q (c t)"),
+            )
+
+        def quantise_positions(c):
+            grouped_words = x_grouped[c][:].bitcast(F32)
+            for j in range(CHUNK_BLOCKS):
+                words = x_raw[c][:, j, :].bitcast(F32)
+                flipped = psum_plain.tile([P, PASSES * 2, P], F32, tag="plain")
+                for gu in range(PASSES * 2):
+                    nc.tensor.transpose(
+                        out=flipped[:, gu, :], in_=words[:, (gu // 2) * 2 * P + gu % 2 : (gu // 2 + 1) * 2 * P : 2], identity=ident[:]
+                    )
+                nc.vector.tensor_copy(
+                    out=grouped_words[:, :, j * P : (j + 1) * P, :],
+                    in_=flipped[:].rearrange("q (g u) s -> q g s u", u=2),
+                )
+            for g in range(PASSES):
+                nc.vector.quantize_mx(
+                    out=x_codes[c][:, g, :].bitcast(FP8X4),
+                    scales=x_scales[c][:, g, :],
+                    in_=x_grouped[c][:, g, :, :].rearrange("q s t -> q (s t)"),
+                )
+
+        def multiply_rotated(n, c):
+            products = []
+            for m in range(GROUP_TILES):
+                acc = psum_mx.tile([P, CHUNK], F32, tag="acc")
+                for g in range(PASSES):
+                    nc.tensor.matmul_mx(
+                        out=acc[:],
+                        lhsT=w_codes[n][:, g, m * P : (m + 1) * P].bitcast(FP8X4),
+                        lhsT_scale=w_scales[n][:, g, m * P : (m + 1) * P],
+                        rhs=x_codes[c][:, g, :].bitcast(FP8X4),
+                        rhs_scale=x_scales[c][:, g, :],
+                        start=(g == 0),
+                        stop=(g == PASSES - 1),
+                    )
+                tile_index = n * GROUP_TILES + m
+                by_cos = work.tile([P, CHUNK], F32, tag="by_cos", bufs=2 * GROUP_TILES)
+                by_sin = work.tile([P, CHUNK], F32, tag="by_sin", bufs=2 * GROUP_TILES)
+                for product, table_t in ((by_cos, cos_t), (by_sin, sin_t)):
+                    nc.vector.scalar_tensor_tensor(
+                        out=product[:],
+                        in0=acc[:],
+                        scalar=bias_cols[:, tile_index : tile_index + 1],
+                        in1=table_t[:, c, :],
+                        op0=ADD,
+                        op1=MULT,
+                    )
+                products.append((by_cos, by_sin))
+            return products
+
+        def finish_rotated(n, c, products):
+            for first in range(0, CHUNK_BLOCKS, PAIR):
+                rotated = work.tile([P, PAIR, GROUP], F32, tag="result")
+                for jj in range(PAIR):
+                    block = slice((first + jj) * P, (first + jj + 1) * P)
+                    total = psum_plain.tile([P, GROUP], F32, tag="plain")
+                    for m in range(GROUP_TILES):
+                        by_cos, by_sin = products[m]
+                        nc.tensor.matmul(
+                            out=total[:, m * P : (m + 1) * P],
+                            lhsT=by_cos[:, block],
+                            rhs=ident[:],
+                            is_transpose=True,
+                            start=True,
+                            stop=False,
+                        )
+                        nc.tensor.matmul(
+                            out=total[:, m * P : (m + 1) * P],
+                            lhsT=by_sin[:, block],
+                            rhs=swap[:],
+                            is_transpose=True,
+                            start=False,
+                            stop=True,
+                        )
+                    nc.scalar.copy(out=rotated[:, jj, :], in_=total[:])
+                store(n, c * CHUNK_BLOCKS + first, rotated)
+
+        def project_plain(n, c):
+            for first in range(0, CHUNK_BLOCKS, PAIR):
+                plain = work.tile([P, PAIR, GROUP], F32, tag="result")
+                for jj in range(PAIR):
+                    block = slice((first + jj) * P, (first + jj + 1) * P)
+                    acc = psum_mx.tile([P, GROUP], F32, tag="acc")
+                    for g in range(PASSES):
+                        nc.tensor.matmul_mx(
+                            out=acc[:],
+                            lhsT=x_codes[c][:, g, block].bitcast(FP8X4),
+                            lhsT_scale=x_scales[c][:, g, block],
+                            rhs=w_codes[n][:, g, :].bitcast(FP8X4),
+                            rhs_scale=w_scales[n][:, g, :],
+                            start=(g == 0),
+                            stop=(g == PASSES - 1),
+                        )
+                    col = (n - ROTATED_GROUPS) * GROUP
+                    nc.vector.tensor_tensor(
+                        out=plain[:, jj, :], in0=acc[:], in1=v_bias[:, col : col + GROUP], op=ADD
+                    )
+                store(n, c * CHUNK_BLOCKS + first, plain)
+
+        def store(n, first_block, result):
+            which, col = divmod(n * GROUP, WIDTH)
+            nc.sync.dma_start(
+                out=out_rows[which][:, first_block : first_block + PAIR, col : col + GROUP],
+                in_=result[:],
+            )
+
+        def quantise_ahead(unit):
+            assert PASSES == CHUNKS
+            step = unit + PASSES
+            if step < GROUPS * PASSES:
+                quantise_weights(step // PASSES, step % PASSES)
+
+        for g in range(PASSES):
+            quantise_weights(0, g)
+        quantise_positions(0)
+        waiting = None
+        for n in range(ROTATED_GROUPS):
+            for c in range(CHUNKS):
+                if n == 0 and c > 0:
+                    quantise_positions(c)
+                quantise_ahead(n * CHUNKS + c)
+                products = multiply_rotated(n, c)
+                if waiting is not None:
+                    finish_rotated(*waiting)
+                waiting = (n, c, products)
+        finish_rotated(*waiting)
+
+        ones = const.tile([P, P], BF16)
+        nc.vector.memset(ones[:], 1.0)
+        v_bias = const.tile([P, WIDTH], F32)
+        for n in range(WIDTH // GROUP):
+            spread = psum_plain.tile([P, GROUP], F32, tag="plain")
+            nc.tensor.matmul(
+                out=spread[:],
+                lhsT=ones[:],
+                rhs=v_bias_row[:, n * GROUP : (n + 1) * GROUP],
+                start=True,
+                stop=True,
+            )
+            nc.scalar.copy(out=v_bias[:, n * GROUP : (n + 1) * GROUP], in_=spread[:])
+        for n in range(ROTATED_GROUPS, GROUPS):
+            for c in range(CHUNKS):
+                quantise_ahead(n * CHUNKS + c)
+                project_plain(n, c)

@@ -31,6 +31,12 @@ PAIR = 2
 
 FLOPS = 2 * S * E * 3 * WIDTH
 
+ORDER = (4, 0, 1, 2, 3, 5)
+V_GPSIMD = ()
+TILES = GROUP_TILES // 2
+HALF_GROUP = TILES * P
+IDENTITY = mybir.ActivationFunctionType.Identity
+
 
 def tile_arlowvisionattention_pa_kernel(
     tc, hidden_states, cos, sin, w_qkv, b_qkv, out_0, out_1, out_2
@@ -40,20 +46,18 @@ def tile_arlowvisionattention_pa_kernel(
         const = ctx.enter_context(tc.tile_pool(name="const", bufs=1))
         operands = ctx.enter_context(tc.tile_pool(name="operands", bufs=1))
         work = ctx.enter_context(tc.tile_pool(name="work", bufs=3))
-        psum_mx = ctx.enter_context(tc.psum_pool(name="psum_mx", bufs=5))
-        psum_plain = ctx.enter_context(tc.psum_pool(name="psum_plain", bufs=3))
+        psum_mx = ctx.enter_context(tc.psum_pool(name="psum_mx", bufs=4))
+        psum_plain = ctx.enter_context(tc.psum_pool(name="psum_plain", bufs=4))
 
         x_rows = hidden_states.rearrange("(p b) k -> p b k", b=S_BLOCKS)
         out_rows = [
             out.rearrange("(p b) h d -> p b (h d)", b=S_BLOCKS) for out in (out_0, out_1, out_2)
         ]
 
-        x_raw = [
-            operands.tile([P, CHUNK_BLOCKS, E], BF16, name="x_raw%d" % c) for c in range(CHUNKS)
-        ]
+        x_raw = [operands.tile([P, PAIR, E], BF16, name="x_raw%d" % i) for i in range(S_BLOCKS // PAIR)]
         x_grouped = [
-            operands.tile([P, PASSES, CHUNK, PACK], BF16, name="x_grouped%d" % c, align_bytes=64)
-            for c in range(CHUNKS)
+            operands.tile([P, PASSES, PAIR * P, PACK], BF16, name="x_grouped%d" % i, align_bytes=64)
+            for i in range(S_BLOCKS // PAIR)
         ]
         x_codes = [
             operands.tile([P, PASSES, CHUNK], U32, name="x_codes%d" % c, align_bytes=64)
@@ -75,246 +79,357 @@ def tile_arlowvisionattention_pa_kernel(
             for n in range(GROUPS)
         ]
 
+        def load_weights(n, g):
+            nc.sync.dma_start(
+                out=w_raw[n][:, g, :, :],
+                in_=w_qkv[
+                    g * K_PASS : (g + 1) * K_PASS, n * GROUP : (n + 1) * GROUP
+                ].rearrange("(q t) n -> q t n", t=PACK),
+            )
+
+        def load_positions(i):
+            nc.sync.dma_start(out=x_raw[i][:], in_=x_rows[:, i * PAIR : (i + 1) * PAIR, :])
+
         cos_raw = const.tile([P, S_BLOCKS, DH], BF16)
         sin_raw = const.tile([P, S_BLOCKS, DH], BF16)
-        nc.scalar.dma_start(out=cos_raw[:], in_=cos.rearrange("(p b) d -> p b d", b=S_BLOCKS))
-        nc.scalar.dma_start(out=sin_raw[:], in_=sin.rearrange("(p b) d -> p b d", b=S_BLOCKS))
-
         rotated_tiles = ROTATED_GROUPS * GROUP_TILES
         bias_rows = const.tile([P, P], BF16)
-        nc.vector.memset(bias_rows[:], 0.0)
+        v_bias_row = const.tile([P, WIDTH], BF16)
+        ones = const.tile([P, P], BF16)
+        ident = const.tile([P, P], F32)
+        ident_bf16 = const.tile([P, P], BF16)
+        swap = const.tile([P, P], F32)
+        warm = const.tile([P, 1], F32)
+        bias_cols = const.tile([P, rotated_tiles], F32)
+        v_bias = const.tile([P, WIDTH], F32)
+        spread_cos = const.tile([P, S_BLOCKS, TILE_HEADS, DH], BF16)
+        spread_sin = const.tile([P, S_BLOCKS, TILE_HEADS, DH], BF16)
+        sin_signed = const.tile([P, S_BLOCKS, DH], BF16)
+        sin_crossed = const.tile([P, S_BLOCKS, DH], BF16)
+        table_t = const.tile([P, 2, CHUNKS * CHUNK], BF16)
+
+        schedule = tc.manual_schedule()
+        ctx.enter_context(schedule)
+
+        nc.gpsimd.memset(warm[:], 0.0)
+        nc.gpsimd.memset(bias_rows[:], 0.0)
+        nc.gpsimd.memset(v_bias_row[:], 0.0)
+        make_identity(nc, ident[:])
+        nc.gpsimd.memset(ones[:], 1.0)
+        warm_out = const.tile([P, 1], F32)
+        nc.scalar.copy(out=warm_out[:], in_=warm[:])
+
+        first = ORDER[0]
+        second = ORDER[1]
+        load_weights(first, 0)
+        load_positions(0)
         nc.scalar.dma_start(
             out=bias_rows[0:rotated_tiles, :],
             in_=b_qkv[0 : rotated_tiles * P].rearrange("(t n) -> t n", n=P),
         )
-        v_bias_row = const.tile([P, WIDTH], BF16)
-        nc.vector.memset(v_bias_row[:], 0.0)
         nc.scalar.dma_start(
             out=v_bias_row[0:1, :],
             in_=b_qkv[2 * WIDTH : 3 * WIDTH].rearrange("(o n) -> o n", o=1),
         )
-
-        def load_weights(n):
+        load_weights(first, 1)
+        load_positions(1)
+        nc.scalar.dma_start(out=cos_raw[:], in_=cos.rearrange("(p b) d -> p b d", b=S_BLOCKS))
+        nc.scalar.dma_start(out=sin_raw[:], in_=sin.rearrange("(p b) d -> p b d", b=S_BLOCKS))
+        for i in range(2, S_BLOCKS // PAIR):
+            load_positions(i)
+        for n in ORDER[1:]:
             for g in range(PASSES):
-                nc.sync.dma_start(
-                    out=w_raw[n][:, g, :, :],
-                    in_=w_qkv[
-                        g * K_PASS : (g + 1) * K_PASS, n * GROUP : (n + 1) * GROUP
-                    ].rearrange("(q t) n -> q t n", t=PACK),
-                )
+                load_weights(n, g)
 
-        load_weights(0)
-        for c in range(CHUNKS):
-            nc.sync.dma_start(
-                out=x_raw[c][:], in_=x_rows[:, c * CHUNK_BLOCKS : (c + 1) * CHUNK_BLOCKS, :]
-            )
-        for n in range(1, GROUPS):
-            load_weights(n)
-
-        ident = const.tile([P, P], F32)
-        make_identity(nc, ident[:])
-        swap = const.tile([P, P], F32)
         swap_pairs = swap[:].rearrange("r (i two) -> r i two", two=2)
         ident_pairs = ident[:].rearrange("r (i two) -> r i two", two=2)
+        nc.vector.tensor_copy(out=ident_bf16[:], in_=ident[:])
         for two in range(2):
             nc.vector.tensor_copy(out=swap_pairs[:, :, two], in_=ident_pairs[:, :, 1 - two])
 
-        bias_rows_f32 = const.tile([P, P], F32)
-        nc.vector.tensor_copy(out=bias_rows_f32[:], in_=bias_rows[:])
-        bias_flipped = psum_plain.tile([P, P], F32, tag="plain")
-        nc.tensor.transpose(out=bias_flipped[:], in_=bias_rows_f32[:], identity=ident[:])
-        bias_cols = const.tile([P, rotated_tiles], F32)
-        nc.vector.tensor_copy(out=bias_cols[:], in_=bias_flipped[:, 0:rotated_tiles])
-
-        own_factor = const.tile([P, S_BLOCKS, TILE_HEADS, DH], F32)
-        nc.vector.tensor_copy(
-            out=own_factor[:],
-            in_=cos_raw[:].unsqueeze(2).to_broadcast([P, S_BLOCKS, TILE_HEADS, DH]),
-        )
-        sin_pairs = sin_raw[:].rearrange("p b (i two) -> p b i two", two=2)
-        crossed = const.tile([P, S_BLOCKS, HALF, 2], F32)
-        nc.vector.tensor_copy(out=crossed[:, :, :, 0], in_=sin_pairs[:, :, :, 1])
-        nc.vector.tensor_scalar_mul(out=crossed[:, :, :, 1], in0=sin_pairs[:, :, :, 0], scalar1=-1.0)
-        neighbour_factor = const.tile([P, S_BLOCKS, TILE_HEADS, DH], F32)
-        nc.vector.tensor_copy(
-            out=neighbour_factor[:],
-            in_=crossed[:]
-            .rearrange("p b i two -> p b (i two)")
-            .unsqueeze(2)
-            .to_broadcast([P, S_BLOCKS, TILE_HEADS, DH]),
-        )
-
-        def flip_table(table, c):
-            flipped = psum_plain.tile([P, CHUNK_BLOCKS, P], F32, tag="plain")
-            for j in range(CHUNK_BLOCKS):
-                nc.tensor.transpose(
-                    out=flipped[:, j, :],
-                    in_=table[:, c * CHUNK_BLOCKS + j, :, :].rearrange("p h d -> p (h d)"),
-                    identity=ident[:],
+        def spread_tables():
+            sin_pairs = sin_raw[:].rearrange("p b (i two) -> p b i two", two=2)
+            for two, sign in ((0, -1.0), (1, 1.0)):
+                nc.vector.tensor_scalar_mul(
+                    out=sin_signed[:].rearrange("p b (i two) -> p b i two", two=2)[:, :, :, two],
+                    in0=sin_pairs[:, :, :, two], scalar1=sign,
                 )
-            return flipped
+            for two in range(2):
+                nc.vector.tensor_copy(
+                    out=sin_crossed[:].rearrange("p b (i two) -> p b i two", two=2)[:, :, :, two],
+                    in_=sin_signed[:].rearrange("p b (i two) -> p b i two", two=2)[:, :, :, 1 - two],
+                )
+            for spread, table in ((spread_cos, cos_raw), (spread_sin, sin_crossed)):
+                nc.vector.tensor_copy(
+                    out=spread[:], in_=table[:].unsqueeze(2).to_broadcast([P, S_BLOCKS, TILE_HEADS, DH])
+                )
 
-        cos_t = const.tile([P, CHUNKS, CHUNK], F32)
-        sin_t = const.tile([P, CHUNKS, CHUNK], F32)
-        for c in range(CHUNKS):
-            for table, table_t in ((own_factor, cos_t), (neighbour_factor, sin_t)):
+        def flip_tables(c):
+            for i, table in enumerate((spread_cos, spread_sin)):
+                flipped = psum_plain.tile([P, CHUNK_BLOCKS, P], BF16, tag="plain")
+                for j in range(CHUNK_BLOCKS):
+                    nc.tensor.transpose(
+                        out=flipped[:, j, :],
+                        in_=table[:, c * CHUNK_BLOCKS + j, :, :].rearrange("p h d -> p (h d)"),
+                        identity=ident_bf16[:],
+                    )
                 nc.scalar.copy(
-                    out=table_t[:, c, :],
-                    in_=flip_table(table, c)[:].rearrange("r j p -> r (j p)"),
+                    out=table_t[:, i, c * CHUNK : (c + 1) * CHUNK],
+                    in_=flipped[:].rearrange("r j p -> r (j p)"),
+                )
+
+        def flip_bias():
+            flipped = psum_plain.tile([P, P], BF16, tag="plain")
+            nc.tensor.transpose(out=flipped[:], in_=bias_rows[:], identity=ident_bf16[:])
+            nc.vector.tensor_copy(out=bias_cols[:], in_=flipped[:, 0:rotated_tiles])
+
+        def spread_v_bias():
+            for n in range(WIDTH // GROUP):
+                spread = psum_plain.tile([P, GROUP], F32, tag="plain")
+                nc.tensor.matmul(
+                    out=spread[:], lhsT=ones[:], rhs=v_bias_row[:, n * GROUP : (n + 1) * GROUP],
+                    start=True, stop=True,
+                )
+                nc.scalar.copy(out=v_bias[:, n * GROUP : (n + 1) * GROUP], in_=spread[:])
+
+        grouped = {}
+
+        def group_weights(n, g, engine, part, parts):
+            if part == 0:
+                w_grouped = work.tile([P, GROUP, PACK], BF16, align_bytes=64, tag="w_grouped")
+                grouped[n, g] = w_grouped
+            cols = slice(part * GROUP // parts, (part + 1) * GROUP // parts)
+            if engine == "S":
+                nc.scalar.copy(
+                    out=grouped[n, g][:, cols, :].rearrange("q (c i) t -> q c t i", i=4),
+                    in_=w_raw[n][:, g, :, cols].rearrange("q t (c i) -> q c t i", i=4),
+                )
+            else:
+                nc.vector.tensor_copy(
+                    out=grouped[n, g][:, cols, :], in_=w_raw[n][:, g, :, cols].rearrange("q t c -> q c t")
                 )
 
         def quantise_weights(n, g):
-            grouped = work.tile([P, GROUP, PACK], BF16, align_bytes=64, tag="w_grouped")
-            nc.scalar.copy(
-                out=grouped[:].rearrange("q (c i) t -> q c t i", i=4),
-                in_=w_raw[n][:, g, :, :].rearrange("q t (c i) -> q c t i", i=4),
-            )
             nc.vector.quantize_mx(
                 out=w_codes[n][:, g, :].bitcast(FP8X4),
                 scales=w_scales[n][:, g, :],
-                in_=grouped[:].rearrange("q c t -> q (c t)"),
+                in_=grouped[n, g][:].rearrange("q c t -> q (c t)"),
             )
 
-        def quantise_positions(c):
-            grouped_words = x_grouped[c][:].bitcast(F32)
-            for j in range(CHUNK_BLOCKS):
-                words = x_raw[c][:, j, :].bitcast(F32)
-                flipped = psum_plain.tile([P, PASSES * 2, P], F32, tag="plain")
-                for gu in range(PASSES * 2):
+        def flip_positions(b, engine):
+            words = x_raw[b // PAIR][:, b % PAIR, :].bitcast(F32)
+            flipped = psum_plain.tile([P, PASSES, 2, P], F32, tag="plain")
+            for g in range(PASSES):
+                for u in range(2):
                     nc.tensor.transpose(
-                        out=flipped[:, gu, :], in_=words[:, (gu // 2) * 2 * P + gu % 2 : (gu // 2 + 1) * 2 * P : 2], identity=ident[:]
+                        out=flipped[:, g, u, :],
+                        in_=words[:, g * 2 * P + u : (g + 1) * 2 * P : 2],
+                        identity=ident[:],
                     )
-                nc.vector.tensor_copy(
-                    out=grouped_words[:, :, j * P : (j + 1) * P, :],
-                    in_=flipped[:].rearrange("q (g u) s -> q g s u", u=2),
-                )
+            copy = nc.scalar.copy if engine == "S" else nc.vector.tensor_copy
+            col = (b % PAIR) * P
+            copy(
+                out=x_grouped[b // PAIR][:].bitcast(F32)[:, :, col : col + P, :],
+                in_=flipped[:].rearrange("q g u s -> q g s u"),
+            )
+
+        def quantise_positions(i):
+            c, col = divmod(i * PAIR * P, CHUNK)
             for g in range(PASSES):
                 nc.vector.quantize_mx(
-                    out=x_codes[c][:, g, :].bitcast(FP8X4),
-                    scales=x_scales[c][:, g, :],
-                    in_=x_grouped[c][:, g, :, :].rearrange("q s t -> q (s t)"),
+                    out=x_codes[c][:, g, col : col + PAIR * P].bitcast(FP8X4),
+                    scales=x_scales[c][:, g, col : col + PAIR * P],
+                    in_=x_grouped[i][:, g, :, :].rearrange("q s t -> q (s t)"),
                 )
 
-        def multiply_rotated(n, c):
-            products = []
-            for m in range(GROUP_TILES):
-                acc = psum_mx.tile([P, CHUNK], F32, tag="acc")
-                for g in range(PASSES):
-                    nc.tensor.matmul_mx(
-                        out=acc[:],
-                        lhsT=w_codes[n][:, g, m * P : (m + 1) * P].bitcast(FP8X4),
-                        lhsT_scale=w_scales[n][:, g, m * P : (m + 1) * P],
-                        rhs=x_codes[c][:, g, :].bitcast(FP8X4),
-                        rhs_scale=x_scales[c][:, g, :],
-                        start=(g == 0),
-                        stop=(g == PASSES - 1),
-                    )
-                tile_index = n * GROUP_TILES + m
-                by_cos = work.tile([P, CHUNK], F32, tag="by_cos", bufs=2 * GROUP_TILES)
-                by_sin = work.tile([P, CHUNK], F32, tag="by_sin", bufs=2 * GROUP_TILES)
-                for product, table_t in ((by_cos, cos_t), (by_sin, sin_t)):
-                    nc.vector.scalar_tensor_tensor(
-                        out=product[:],
-                        in0=acc[:],
-                        scalar=bias_cols[:, tile_index : tile_index + 1],
-                        in1=table_t[:, c, :],
-                        op0=ADD,
-                        op1=MULT,
-                    )
-                products.append((by_cos, by_sin))
-            return products
+        results = {}
 
-        def finish_rotated(n, c, products):
-            for first in range(0, CHUNK_BLOCKS, PAIR):
-                rotated = work.tile([P, PAIR, GROUP], F32, tag="result")
-                for jj in range(PAIR):
-                    block = slice((first + jj) * P, (first + jj + 1) * P)
-                    total = psum_plain.tile([P, GROUP], F32, tag="plain")
-                    for m in range(GROUP_TILES):
-                        by_cos, by_sin = products[m]
-                        nc.tensor.matmul(
-                            out=total[:, m * P : (m + 1) * P],
-                            lhsT=by_cos[:, block],
-                            rhs=ident[:],
-                            is_transpose=True,
-                            start=True,
-                            stop=False,
-                        )
-                        nc.tensor.matmul(
-                            out=total[:, m * P : (m + 1) * P],
-                            lhsT=by_sin[:, block],
-                            rhs=swap[:],
-                            is_transpose=True,
-                            start=False,
-                            stop=True,
-                        )
-                    nc.scalar.copy(out=rotated[:, jj, :], in_=total[:])
-                store(n, c * CHUNK_BLOCKS + first, rotated)
-
-        def project_plain(n, c):
-            for first in range(0, CHUNK_BLOCKS, PAIR):
-                plain = work.tile([P, PAIR, GROUP], F32, tag="result")
-                for jj in range(PAIR):
-                    block = slice((first + jj) * P, (first + jj + 1) * P)
-                    acc = psum_mx.tile([P, GROUP], F32, tag="acc")
-                    for g in range(PASSES):
-                        nc.tensor.matmul_mx(
-                            out=acc[:],
-                            lhsT=x_codes[c][:, g, block].bitcast(FP8X4),
-                            lhsT_scale=x_scales[c][:, g, block],
-                            rhs=w_codes[n][:, g, :].bitcast(FP8X4),
-                            rhs_scale=w_scales[n][:, g, :],
-                            start=(g == 0),
-                            stop=(g == PASSES - 1),
-                        )
-                    col = (n - ROTATED_GROUPS) * GROUP
-                    nc.vector.tensor_tensor(
-                        out=plain[:, jj, :], in0=acc[:], in1=v_bias[:, col : col + GROUP], op=ADD
-                    )
-                store(n, c * CHUNK_BLOCKS + first, plain)
-
-        def store(n, first_block, result):
+        def store(n, c, pair):
             which, col = divmod(n * GROUP, WIDTH)
+            first_block = c * CHUNK_BLOCKS + pair * PAIR
             nc.sync.dma_start(
                 out=out_rows[which][:, first_block : first_block + PAIR, col : col + GROUP],
-                in_=result[:],
+                in_=results[n, c, pair][:],
             )
 
-        def quantise_ahead(unit):
-            assert PASSES == CHUNKS
-            step = unit + PASSES
-            if step < GROUPS * PASSES:
-                quantise_weights(step // PASSES, step % PASSES)
+        products = {}
+        accs = {}
 
-        for g in range(PASSES):
-            quantise_weights(0, g)
+        def multiply(n, c, m):
+            acc = psum_mx.tile([P, GROUP], F32, tag="acc")
+            accs[n, c, m] = acc
+            mine = slice(m * P, (m + 1) * P)
+            for g in range(PASSES):
+                if n < ROTATED_GROUPS:
+                    lhs, rhs, lcols, rcols = (w_codes[n], w_scales[n]), (x_codes[c], x_scales[c]), mine, slice(0, CHUNK)
+                else:
+                    lhs, rhs, lcols, rcols = (x_codes[c], x_scales[c]), (w_codes[n], w_scales[n]), mine, slice(0, GROUP)
+                nc.tensor.matmul_mx(
+                    out=acc[:],
+                    lhsT=lhs[0][:, g, lcols].bitcast(FP8X4),
+                    lhsT_scale=lhs[1][:, g, lcols],
+                    rhs=rhs[0][:, g, rcols].bitcast(FP8X4),
+                    rhs_scale=rhs[1][:, g, rcols],
+                    start=(g == 0),
+                    stop=(g == PASSES - 1),
+                )
+
+        def emit_transposed(n, c, m):
+            acc = accs[n, c, m]
+            tile_index = n * GROUP_TILES + m
+            bias = bias_cols[:, tile_index : tile_index + 1]
+            if m < TILES:
+                both = work.tile([P, 2, CHUNK], F32, tag="both", bufs=2 * TILES + 1)
+                nc.vector.scalar_tensor_tensor(
+                    out=both[:],
+                    in0=acc[:].unsqueeze(1).to_broadcast([P, 2, CHUNK]),
+                    scalar=bias,
+                    in1=table_t[:, :, c * CHUNK : (c + 1) * CHUNK],
+                    op0=ADD,
+                    op1=MULT,
+                )
+                products[n, c, m] = both
+            else:
+                biased = work.tile([P, CHUNK], F32, tag="biased", bufs=2 * TILES + 1)
+                nc.scalar.activation(out=biased[:], in_=acc[:], func=IDENTITY, bias=bias, scale=1.0)
+                products[n, c, m] = biased
+
+        banks = {}
+
+        def flip_back(n, c, pair):
+            summed = psum_plain.tile([P, PAIR, HALF_GROUP], F32, tag="plain")
+            bare = psum_plain.tile([P, PAIR, HALF_GROUP], F32, tag="plain")
+            banks[n, c, pair] = (summed, bare)
+            result = work.tile([P, PAIR, GROUP], F32, tag="result", bufs=8)
+            results[n, c, pair] = result
+            for jj in range(PAIR):
+                block = slice((pair * PAIR + jj) * P, (pair * PAIR + jj + 1) * P)
+                for m in range(TILES):
+                    for i, order in enumerate((ident, swap)):
+                        nc.tensor.matmul(
+                            out=summed[:, jj, m * P : (m + 1) * P],
+                            lhsT=products[n, c, m][:, i, block],
+                            rhs=order[:],
+                            is_transpose=True,
+                            start=(i == 0),
+                            stop=(i == 1),
+                        )
+            for jj in range(PAIR):
+                block = slice((pair * PAIR + jj) * P, (pair * PAIR + jj + 1) * P)
+                for m in range(TILES):
+                    nc.tensor.transpose(
+                        out=bare[:, jj, m * P : (m + 1) * P], in_=products[n, c, TILES + m][:, block], identity=ident[:]
+                    )
+
+        def finish_summed(n, c, pair):
+            summed, bare = banks[n, c, pair]
+            nc.scalar.copy(out=results[n, c, pair][:, :, 0:HALF_GROUP], in_=summed[:])
+
+        def finish_bare(n, c, pair, between):
+            summed, bare = banks[n, c, pair]
+            blocks = slice(c * CHUNK_BLOCKS + pair * PAIR, c * CHUNK_BLOCKS + (pair + 1) * PAIR)
+            heads = HALF_GROUP // DH
+            by_cos = work.tile([P, PAIR, HALF_GROUP], F32, tag="by_cos", bufs=2)
+            by_sin = work.tile([P, PAIR, HALF_GROUP], F32, tag="by_sin", bufs=2)
+            nc.vector.tensor_tensor(
+                out=by_cos[:].rearrange("p b (h d) -> p b h d", d=DH),
+                in0=bare[:].rearrange("p b (h d) -> p b h d", d=DH),
+                in1=cos_raw[:, blocks, :].unsqueeze(2).to_broadcast([P, PAIR, heads, DH]),
+                op=MULT,
+            )
+            if between:
+                quantise_weights(*between)
+            nc.vector.tensor_tensor(
+                out=by_sin[:].rearrange("p b (h i two) -> p b h i two", h=heads, two=2),
+                in0=bare[:].rearrange("p b (h i two) -> p b h i two", h=heads, two=2)[:, :, :, :, ::-1],
+                in1=sin_signed[:, blocks, :].rearrange("p b (i two) -> p b i two", two=2).unsqueeze(2).to_broadcast([P, PAIR, heads, HALF, 2]),
+                op=MULT,
+            )
+            nc.gpsimd.tensor_tensor(
+                out=results[n, c, pair][:, :, HALF_GROUP:GROUP], in0=by_cos[:], in1=by_sin[:], op=ADD
+            )
+
+        def emit_plain(n, c, m):
+            acc = accs[n, c, m]
+            pair = m // PAIR
+            if m % PAIR == 0:
+                result = work.tile([P, PAIR, GROUP], F32, tag="result", bufs=8)
+                results[n, c, pair] = result
+            row = results[n, c, pair][:, m % PAIR, :]
+            col = (n - ROTATED_GROUPS) * GROUP
+            if m in V_GPSIMD:
+                copied = work.tile([P, GROUP], F32, tag="copied", bufs=2)
+                nc.scalar.copy(out=copied[:], in_=acc[:])
+                nc.gpsimd.tensor_tensor(out=row, in0=copied[:], in1=v_bias[:, col : col + GROUP], op=ADD)
+            else:
+                nc.vector.tensor_tensor(out=row, in0=acc[:], in1=v_bias[:, col : col + GROUP], op=ADD)
+            if m % PAIR == PAIR - 1:
+                store(n, c, pair)
+
+        def multiply_pair(n, c, pair):
+            for m in (2 * pair, 2 * pair + 1):
+                multiply(n, c, m)
+
+        def emit_pair(n, c, pair):
+            for m in (2 * pair, 2 * pair + 1):
+                emit_plain(n, c, m)
+
+        group_weights(first, 0, "V", 0, 1)
+        flip_positions(0, "S")
+        flip_positions(1, "S")
+        quantise_weights(first, 0)
+        group_weights(first, 1, "V", 0, 1)
         quantise_positions(0)
-        waiting = None
-        for n in range(ROTATED_GROUPS):
-            for c in range(CHUNKS):
-                if n == 0 and c > 0:
-                    quantise_positions(c)
-                quantise_ahead(n * CHUNKS + c)
-                products = multiply_rotated(n, c)
-                if waiting is not None:
-                    finish_rotated(*waiting)
-                waiting = (n, c, products)
-        finish_rotated(*waiting)
-
-        ones = const.tile([P, P], BF16)
-        nc.vector.memset(ones[:], 1.0)
-        v_bias = const.tile([P, WIDTH], F32)
-        for n in range(WIDTH // GROUP):
-            spread = psum_plain.tile([P, GROUP], F32, tag="plain")
-            nc.tensor.matmul(
-                out=spread[:],
-                lhsT=ones[:],
-                rhs=v_bias_row[:, n * GROUP : (n + 1) * GROUP],
-                start=True,
-                stop=True,
-            )
-            nc.scalar.copy(out=v_bias[:, n * GROUP : (n + 1) * GROUP], in_=spread[:])
-        for n in range(ROTATED_GROUPS, GROUPS):
-            for c in range(CHUNKS):
-                quantise_ahead(n * CHUNKS + c)
-                project_plain(n, c)
+        quantise_weights(first, 1)
+        spread_v_bias()
+        flip_bias()
+        flip_positions(2, "S")
+        flip_positions(3, "S")
+        multiply_pair(first, 0, 0)
+        spread_tables()
+        quantise_positions(1)
+        emit_pair(first, 0, 0)
+        flip_positions(4, "S")
+        flip_positions(5, "S")
+        multiply_pair(first, 0, 1)
+        quantise_positions(2)
+        emit_pair(first, 0, 1)
+        flip_positions(6, "S")
+        flip_positions(7, "S")
+        group_weights(second, 1, "S", 0, 2)
+        group_weights(second, 1, "S", 1, 2)
+        multiply_pair(first, 1, 0)
+        quantise_positions(3)
+        group_weights(second, 0, "V", 0, 1)
+        emit_pair(first, 1, 0)
+        flip_tables(0)
+        quantise_weights(second, 0)
+        multiply_pair(first, 1, 1)
+        quantise_weights(second, 1)
+        emit_pair(first, 1, 1)
+        flip_tables(1)
+        units = [(n, c) for n in ORDER[1:] for c in range(CHUNKS)]
+        pieces = [(n, g) for n in ORDER[2:] for g in range(PASSES)]
+        previous = None
+        for part in range(2):
+            group_weights(*pieces[0], "S", part, 2)
+        for i, (n, c) in enumerate(units):
+            rotated = n < ROTATED_GROUPS
+            for pair in range(2):
+                mine = (pair, TILES + pair) if rotated else (2 * pair, 2 * pair + 1)
+                for m in mine:
+                    multiply(n, c, m)
+                if previous:
+                    flip_back(*previous, pair)
+                for m in mine:
+                    emit_transposed(n, c, m) if rotated else emit_plain(n, c, m)
+                ready = pieces[i] if pair == 0 and i < len(pieces) else None
+                if previous:
+                    finish_summed(*previous, pair)
+                    finish_bare(*previous, pair, ready)
+                    store(*previous, pair)
+                elif ready:
+                    quantise_weights(*ready)
+                if i + 1 < len(pieces):
+                    group_weights(*pieces[i + 1], "S", pair, 2)
+            previous = (n, c) if rotated else None

@@ -32,7 +32,10 @@ PAIR = 2
 FLOPS = 2 * S * E * 3 * WIDTH
 
 ORDER = (4, 0, 1, 2, 3, 5)
-V_GPSIMD = ()
+HALVES = [("R", n, c, pair) for n in range(4) for c in range(2) for pair in range(2)] + [("V", 5, 0, 0), ("F", 3, 1, 0), ("V", 5, 0, 1), ("F", 3, 1, 1), ("V", 5, 1, 0), ("V", 5, 1, 1)]
+S_SEQ = [(1, 1), (2, 0), (2, 1), (3, 0), (3, 1), (5, 0), (5, 1)]
+QUANTISE = {2 * i: piece for i, piece in enumerate([(1, 0)] + S_SEQ)}
+REGROUP = {2 * i + part: [piece + ("S", part, 2)] for i, piece in enumerate(S_SEQ) for part in range(2)}
 TILES = GROUP_TILES // 2
 HALF_GROUP = TILES * P
 IDENTITY = mybir.ActivationFunctionType.Identity
@@ -199,7 +202,12 @@ def tile_arlowvisionattention_pa_kernel(
                 w_grouped = work.tile([P, GROUP, PACK], BF16, align_bytes=64, tag="w_grouped")
                 grouped[n, g] = w_grouped
             cols = slice(part * GROUP // parts, (part + 1) * GROUP // parts)
-            if engine == "S":
+            if engine == "G":
+                nc.gpsimd.tensor_scalar(
+                    out=grouped[n, g][:, cols, :], in0=w_raw[n][:, g, :, cols].rearrange("q t c -> q c t"),
+                    scalar1=1.0, scalar2=0.0, op0=MULT, op1=ADD,
+                )
+            elif engine == "S":
                 nc.scalar.copy(
                     out=grouped[n, g][:, cols, :].rearrange("q (c i) t -> q c t i", i=4),
                     in_=w_raw[n][:, g, :, cols].rearrange("q t (c i) -> q c t i", i=4),
@@ -357,12 +365,7 @@ def tile_arlowvisionattention_pa_kernel(
                 results[n, c, pair] = result
             row = results[n, c, pair][:, m % PAIR, :]
             col = (n - ROTATED_GROUPS) * GROUP
-            if m in V_GPSIMD:
-                copied = work.tile([P, GROUP], F32, tag="copied", bufs=2)
-                nc.scalar.copy(out=copied[:], in_=acc[:])
-                nc.gpsimd.tensor_tensor(out=row, in0=copied[:], in1=v_bias[:, col : col + GROUP], op=ADD)
-            else:
-                nc.vector.tensor_tensor(out=row, in0=acc[:], in1=v_bias[:, col : col + GROUP], op=ADD)
+            nc.vector.tensor_tensor(out=row, in0=acc[:], in1=v_bias[:, col : col + GROUP], op=ADD)
             if m % PAIR == PAIR - 1:
                 store(n, c, pair)
 
@@ -399,8 +402,11 @@ def tile_arlowvisionattention_pa_kernel(
         group_weights(second, 1, "S", 0, 2)
         group_weights(second, 1, "S", 1, 2)
         multiply_pair(first, 1, 0)
+        group_weights(second, 0, "G", 0, 4)
+        group_weights(second, 0, "G", 1, 4)
         quantise_positions(3)
-        group_weights(second, 0, "V", 0, 1)
+        group_weights(second, 0, "G", 2, 4)
+        group_weights(second, 0, "G", 3, 4)
         emit_pair(first, 1, 0)
         flip_tables(0)
         quantise_weights(second, 0)
@@ -408,28 +414,32 @@ def tile_arlowvisionattention_pa_kernel(
         quantise_weights(second, 1)
         emit_pair(first, 1, 1)
         flip_tables(1)
-        units = [(n, c) for n in ORDER[1:] for c in range(CHUNKS)]
-        pieces = [(n, g) for n in ORDER[2:] for g in range(PASSES)]
-        previous = None
-        for part in range(2):
-            group_weights(*pieces[0], "S", part, 2)
-        for i, (n, c) in enumerate(units):
-            rotated = n < ROTATED_GROUPS
-            for pair in range(2):
-                mine = (pair, TILES + pair) if rotated else (2 * pair, 2 * pair + 1)
+        group_weights(1, 0, "S", 0, 2)
+        group_weights(1, 0, "S", 1, 2)
+        for h, step in enumerate(HALVES):
+            kind, n, c, pair = step
+            before = (n, c - 1) if c else (n - 1, 1)
+            rotated = kind == "R"
+            mine = (pair, TILES + pair) if rotated else (2 * pair, 2 * pair + 1)
+            finishing = None
+            if kind == "F":
+                finishing = (n, c)
+            elif kind == "R" and before[0] >= 0:
+                finishing = before
+            if kind != "F":
                 for m in mine:
                     multiply(n, c, m)
-                if previous:
-                    flip_back(*previous, pair)
+            if finishing:
+                flip_back(*finishing, pair)
+            if kind != "F":
                 for m in mine:
                     emit_transposed(n, c, m) if rotated else emit_plain(n, c, m)
-                ready = pieces[i] if pair == 0 and i < len(pieces) else None
-                if previous:
-                    finish_summed(*previous, pair)
-                    finish_bare(*previous, pair, ready)
-                    store(*previous, pair)
-                elif ready:
-                    quantise_weights(*ready)
-                if i + 1 < len(pieces):
-                    group_weights(*pieces[i + 1], "S", pair, 2)
-            previous = (n, c) if rotated else None
+            ready = QUANTISE.get(h)
+            if finishing:
+                finish_summed(*finishing, pair)
+                finish_bare(*finishing, pair, ready)
+                store(*finishing, pair)
+            elif ready:
+                quantise_weights(*ready)
+            for n2, g2, engine, part, parts in REGROUP.get(h, ()):
+                group_weights(n2, g2, engine, part, parts)

@@ -10,6 +10,7 @@ U8 = mybir.dt.uint8
 FP8X4 = mybir.dt.float8_e4m3fn_x4
 ADD = mybir.AluOpType.add
 MULT = mybir.AluOpType.mult
+IDENTITY = mybir.ActivationFunctionType.Identity
 
 S, E, HEADS, DH = 1024, 1024, 16, 64
 WIDTH = HEADS * DH
@@ -26,19 +27,13 @@ GROUP = 512
 GROUPS = 3 * WIDTH // GROUP
 ROTATED_GROUPS = 2 * WIDTH // GROUP
 GROUP_TILES = GROUP // P
-TILE_HEADS = P // DH
-PAIR = 2
-
-FLOPS = 2 * S * E * 3 * WIDTH
-
-ORDER = (4, 0, 1, 2, 3, 5)
-HALVES = [("R", n, c, pair) for n in range(4) for c in range(2) for pair in range(2)] + [("V", 5, 0, 0), ("F", 3, 1, 0), ("V", 5, 0, 1), ("F", 3, 1, 1), ("V", 5, 1, 0), ("V", 5, 1, 1)]
-S_SEQ = [(1, 1), (2, 0), (2, 1), (3, 0), (3, 1), (5, 0), (5, 1)]
-QUANTISE = {2 * i: piece for i, piece in enumerate([(1, 0)] + S_SEQ)}
-REGROUP = {2 * i + part: [piece + ("S", part, 2)] for i, piece in enumerate(S_SEQ) for part in range(2)}
 TILES = GROUP_TILES // 2
 HALF_GROUP = TILES * P
-IDENTITY = mybir.ActivationFunctionType.Identity
+TILE_HEADS = P // DH
+PAIR = 2
+PAIRS = CHUNK_BLOCKS // PAIR
+
+FLOPS = 2 * S * E * 3 * WIDTH
 
 
 def tile_arlowvisionattention_pa_kernel(
@@ -81,6 +76,23 @@ def tile_arlowvisionattention_pa_kernel(
             operands.tile([P, PASSES, GROUP], U8, name="w_scales%d" % n, align_bytes=64)
             for n in range(GROUPS)
         ]
+        cos_raw = const.tile([P, S_BLOCKS, DH], BF16)
+        sin_raw = const.tile([P, S_BLOCKS, DH], BF16)
+        sin_signed = const.tile([P, S_BLOCKS, DH], BF16)
+        rotated_tiles = ROTATED_GROUPS * GROUP_TILES
+        bias_rows = const.tile([P, P], BF16)
+        bias_cols = const.tile([P, rotated_tiles], F32)
+        v_bias = const.tile([P, WIDTH], F32)
+        ident = const.tile([P, P], F32)
+        ident_bf16 = const.tile([P, P], BF16)
+        swap = const.tile([P, P], F32)
+        warm = const.tile([P, 2], F32)
+        spread_cos = const.tile([P, S_BLOCKS, TILE_HEADS, DH], BF16)
+        spread_sin = const.tile([P, S_BLOCKS, TILE_HEADS, DH], BF16)
+        table_t = const.tile([P, 2, CHUNKS * CHUNK], BF16)
+
+        schedule = tc.manual_schedule()
+        ctx.enter_context(schedule)
 
         def load_weights(n, g):
             nc.sync.dma_start(
@@ -93,54 +105,23 @@ def tile_arlowvisionattention_pa_kernel(
         def load_positions(i):
             nc.sync.dma_start(out=x_raw[i][:], in_=x_rows[:, i * PAIR : (i + 1) * PAIR, :])
 
-        cos_raw = const.tile([P, S_BLOCKS, DH], BF16)
-        sin_raw = const.tile([P, S_BLOCKS, DH], BF16)
-        rotated_tiles = ROTATED_GROUPS * GROUP_TILES
-        bias_rows = const.tile([P, P], BF16)
-        v_bias_row = const.tile([P, WIDTH], BF16)
-        ones = const.tile([P, P], BF16)
-        ident = const.tile([P, P], F32)
-        ident_bf16 = const.tile([P, P], BF16)
-        swap = const.tile([P, P], F32)
-        warm = const.tile([P, 1], F32)
-        bias_cols = const.tile([P, rotated_tiles], F32)
-        v_bias = const.tile([P, WIDTH], F32)
-        spread_cos = const.tile([P, S_BLOCKS, TILE_HEADS, DH], BF16)
-        spread_sin = const.tile([P, S_BLOCKS, TILE_HEADS, DH], BF16)
-        sin_signed = const.tile([P, S_BLOCKS, DH], BF16)
-        sin_crossed = const.tile([P, S_BLOCKS, DH], BF16)
-        table_t = const.tile([P, 2, CHUNKS * CHUNK], BF16)
-
-        schedule = tc.manual_schedule()
-        ctx.enter_context(schedule)
-
-        nc.gpsimd.memset(warm[:], 0.0)
+        v_first, v_last = ROTATED_GROUPS, ROTATED_GROUPS + 1
         nc.gpsimd.memset(bias_rows[:], 0.0)
-        nc.gpsimd.memset(v_bias_row[:], 0.0)
+        nc.gpsimd.memset(warm[:], 0.0)
         make_identity(nc, ident[:])
-        nc.gpsimd.memset(ones[:], 1.0)
-        warm_out = const.tile([P, 1], F32)
-        nc.scalar.copy(out=warm_out[:], in_=warm[:])
-
-        first = ORDER[0]
-        second = ORDER[1]
-        load_weights(first, 0)
+        nc.scalar.copy(out=warm[:, 1:2], in_=warm[:, 0:1])
+        load_weights(v_first, 0)
         load_positions(0)
-        nc.scalar.dma_start(
-            out=bias_rows[0:rotated_tiles, :],
-            in_=b_qkv[0 : rotated_tiles * P].rearrange("(t n) -> t n", n=P),
+        nc.sync.dma_start(
+            out=bias_rows[0 : 3 * WIDTH // P, :], in_=b_qkv.rearrange("(t n) -> t n", n=P)
         )
-        nc.scalar.dma_start(
-            out=v_bias_row[0:1, :],
-            in_=b_qkv[2 * WIDTH : 3 * WIDTH].rearrange("(o n) -> o n", o=1),
-        )
-        load_weights(first, 1)
+        load_weights(v_first, 1)
         load_positions(1)
-        nc.scalar.dma_start(out=cos_raw[:], in_=cos.rearrange("(p b) d -> p b d", b=S_BLOCKS))
-        nc.scalar.dma_start(out=sin_raw[:], in_=sin.rearrange("(p b) d -> p b d", b=S_BLOCKS))
-        for i in range(2, S_BLOCKS // PAIR):
-            load_positions(i)
-        for n in ORDER[1:]:
+        nc.sync.dma_start(out=cos_raw[:], in_=cos.rearrange("(p b) d -> p b d", b=S_BLOCKS))
+        nc.sync.dma_start(out=sin_raw[:], in_=sin.rearrange("(p b) d -> p b d", b=S_BLOCKS))
+        load_positions(2)
+        load_positions(3)
+        for n in list(range(ROTATED_GROUPS)) + [v_last]:
             for g in range(PASSES):
                 load_weights(n, g)
 
@@ -152,20 +133,21 @@ def tile_arlowvisionattention_pa_kernel(
 
         def spread_tables():
             sin_pairs = sin_raw[:].rearrange("p b (i two) -> p b i two", two=2)
+            signed_pairs = sin_signed[:].rearrange("p b (i two) -> p b i two", two=2)
+            spread_pairs = spread_sin[:].rearrange("p b h (i two) -> p b h i two", two=2)
             for two, sign in ((0, -1.0), (1, 1.0)):
                 nc.vector.tensor_scalar_mul(
-                    out=sin_signed[:].rearrange("p b (i two) -> p b i two", two=2)[:, :, :, two],
-                    in0=sin_pairs[:, :, :, two], scalar1=sign,
+                    out=signed_pairs[:, :, :, two], in0=sin_pairs[:, :, :, two], scalar1=sign
                 )
-            for two in range(2):
-                nc.vector.tensor_copy(
-                    out=sin_crossed[:].rearrange("p b (i two) -> p b i two", two=2)[:, :, :, two],
-                    in_=sin_signed[:].rearrange("p b (i two) -> p b i two", two=2)[:, :, :, 1 - two],
+                nc.vector.tensor_scalar_mul(
+                    out=spread_pairs[:, :, :, :, 1 - two],
+                    in0=sin_pairs[:, :, :, two].unsqueeze(2).to_broadcast([P, S_BLOCKS, TILE_HEADS, HALF]),
+                    scalar1=sign,
                 )
-            for spread, table in ((spread_cos, cos_raw), (spread_sin, sin_crossed)):
-                nc.vector.tensor_copy(
-                    out=spread[:], in_=table[:].unsqueeze(2).to_broadcast([P, S_BLOCKS, TILE_HEADS, DH])
-                )
+            nc.vector.tensor_copy(
+                out=spread_cos[:],
+                in_=cos_raw[:].unsqueeze(2).to_broadcast([P, S_BLOCKS, TILE_HEADS, DH]),
+            )
 
         def flip_tables(c):
             for i, table in enumerate((spread_cos, spread_sin)):
@@ -188,33 +170,40 @@ def tile_arlowvisionattention_pa_kernel(
 
         def spread_v_bias():
             for n in range(WIDTH // GROUP):
-                spread = psum_plain.tile([P, GROUP], F32, tag="plain")
-                nc.tensor.matmul(
-                    out=spread[:], lhsT=ones[:], rhs=v_bias_row[:, n * GROUP : (n + 1) * GROUP],
-                    start=True, stop=True,
+                spread = psum_plain.tile([P, GROUP_TILES, P], F32, tag="plain")
+                for m in range(GROUP_TILES):
+                    row = rotated_tiles + n * GROUP_TILES + m
+                    nc.tensor.matmul(
+                        out=spread[:, m, :],
+                        lhsT=ident_bf16[:, row : row + 1].to_broadcast([P, P]),
+                        rhs=bias_rows[:],
+                        start=True,
+                        stop=True,
+                    )
+                nc.scalar.copy(
+                    out=v_bias[:, n * GROUP : (n + 1) * GROUP],
+                    in_=spread[:].rearrange("p m n -> p (m n)"),
                 )
-                nc.scalar.copy(out=v_bias[:, n * GROUP : (n + 1) * GROUP], in_=spread[:])
 
         grouped = {}
 
-        def group_weights(n, g, engine, part, parts):
-            if part == 0:
-                w_grouped = work.tile([P, GROUP, PACK], BF16, align_bytes=64, tag="w_grouped")
+        def group_weights(engine, n, g, first, last):
+            if first == 0:
+                w_grouped = work.tile([P, GROUP, PACK], BF16, align_bytes=64, tag="w_grouped", bufs=4)
                 grouped[n, g] = w_grouped
-            cols = slice(part * GROUP // parts, (part + 1) * GROUP // parts)
-            if engine == "G":
-                nc.gpsimd.tensor_scalar(
-                    out=grouped[n, g][:, cols, :], in0=w_raw[n][:, g, :, cols].rearrange("q t c -> q c t"),
-                    scalar1=1.0, scalar2=0.0, op0=MULT, op1=ADD,
-                )
-            elif engine == "S":
+            out = grouped[n, g][:, first:last, :]
+            raw = w_raw[n][:, g, :, first:last]
+            if engine == "scalar":
                 nc.scalar.copy(
-                    out=grouped[n, g][:, cols, :].rearrange("q (c i) t -> q c t i", i=4),
-                    in_=w_raw[n][:, g, :, cols].rearrange("q t (c i) -> q c t i", i=4),
+                    out=out.rearrange("q (c i) t -> q c t i", i=4),
+                    in_=raw.rearrange("q t (c i) -> q c t i", i=4),
                 )
+            elif engine == "vector":
+                nc.vector.tensor_copy(out=out, in_=raw.rearrange("q t c -> q c t"))
             else:
-                nc.vector.tensor_copy(
-                    out=grouped[n, g][:, cols, :], in_=w_raw[n][:, g, :, cols].rearrange("q t c -> q c t")
+                nc.gpsimd.tensor_scalar(
+                    out=out, in0=raw.rearrange("q t c -> q c t"),
+                    scalar1=1.0, scalar2=0.0, op0=MULT, op1=ADD,
                 )
 
         def quantise_weights(n, g):
@@ -224,22 +213,21 @@ def tile_arlowvisionattention_pa_kernel(
                 in_=grouped[n, g][:].rearrange("q c t -> q (c t)"),
             )
 
-        def flip_positions(b, engine):
-            words = x_raw[b // PAIR][:, b % PAIR, :].bitcast(F32)
-            flipped = psum_plain.tile([P, PASSES, 2, P], F32, tag="plain")
-            for g in range(PASSES):
-                for u in range(2):
-                    nc.tensor.transpose(
-                        out=flipped[:, g, u, :],
-                        in_=words[:, g * 2 * P + u : (g + 1) * 2 * P : 2],
-                        identity=ident[:],
-                    )
-            copy = nc.scalar.copy if engine == "S" else nc.vector.tensor_copy
-            col = (b % PAIR) * P
-            copy(
-                out=x_grouped[b // PAIR][:].bitcast(F32)[:, :, col : col + P, :],
-                in_=flipped[:].rearrange("q g u s -> q g s u"),
-            )
+        def flip_positions(i):
+            for j in range(PAIR):
+                words = x_raw[i][:, j, :].bitcast(F32)
+                flipped = psum_plain.tile([P, PASSES, 2, P], F32, tag="plain")
+                for g in range(PASSES):
+                    for u in range(2):
+                        nc.tensor.transpose(
+                            out=flipped[:, g, u, :],
+                            in_=words[:, g * 2 * P + u : (g + 1) * 2 * P : 2],
+                            identity=ident[:],
+                        )
+                nc.scalar.copy(
+                    out=x_grouped[i][:].bitcast(F32)[:, :, j * P : (j + 1) * P, :],
+                    in_=flipped[:].rearrange("q g u s -> q g s u"),
+                )
 
         def quantise_positions(i):
             c, col = divmod(i * PAIR * P, CHUNK)
@@ -251,6 +239,13 @@ def tile_arlowvisionattention_pa_kernel(
                 )
 
         results = {}
+        accs = {}
+        products = {}
+        banks = {}
+
+        def new_result(n, c, pair):
+            result = work.tile([P, PAIR, GROUP], F32, tag="result", bufs=8)
+            results[n, c, pair] = result
 
         def store(n, c, pair):
             which, col = divmod(n * GROUP, WIDTH)
@@ -260,29 +255,27 @@ def tile_arlowvisionattention_pa_kernel(
                 in_=results[n, c, pair][:],
             )
 
-        products = {}
-        accs = {}
-
         def multiply(n, c, m):
             acc = psum_mx.tile([P, GROUP], F32, tag="acc")
             accs[n, c, m] = acc
-            mine = slice(m * P, (m + 1) * P)
+            mine, everything = slice(m * P, (m + 1) * P), slice(0, GROUP)
+            weights, positions = (w_codes[n], w_scales[n]), (x_codes[c], x_scales[c])
+            if n < ROTATED_GROUPS:
+                stationary, moving = weights, positions
+            else:
+                stationary, moving = positions, weights
             for g in range(PASSES):
-                if n < ROTATED_GROUPS:
-                    lhs, rhs, lcols, rcols = (w_codes[n], w_scales[n]), (x_codes[c], x_scales[c]), mine, slice(0, CHUNK)
-                else:
-                    lhs, rhs, lcols, rcols = (x_codes[c], x_scales[c]), (w_codes[n], w_scales[n]), mine, slice(0, GROUP)
                 nc.tensor.matmul_mx(
                     out=acc[:],
-                    lhsT=lhs[0][:, g, lcols].bitcast(FP8X4),
-                    lhsT_scale=lhs[1][:, g, lcols],
-                    rhs=rhs[0][:, g, rcols].bitcast(FP8X4),
-                    rhs_scale=rhs[1][:, g, rcols],
+                    lhsT=stationary[0][:, g, mine].bitcast(FP8X4),
+                    lhsT_scale=stationary[1][:, g, mine],
+                    rhs=moving[0][:, g, everything].bitcast(FP8X4),
+                    rhs_scale=moving[1][:, g, everything],
                     start=(g == 0),
                     stop=(g == PASSES - 1),
                 )
 
-        def emit_transposed(n, c, m):
+        def leave_rotated(n, c, m):
             acc = accs[n, c, m]
             tile_index = n * GROUP_TILES + m
             bias = bias_cols[:, tile_index : tile_index + 1]
@@ -302,144 +295,161 @@ def tile_arlowvisionattention_pa_kernel(
                 nc.scalar.activation(out=biased[:], in_=acc[:], func=IDENTITY, bias=bias, scale=1.0)
                 products[n, c, m] = biased
 
-        banks = {}
+        def leave_plain(n, c, m, by_gpsimd):
+            acc = accs[n, c, m]
+            pair = m // PAIR
+            if m % PAIR == 0:
+                new_result(n, c, pair)
+            row = results[n, c, pair][:, m % PAIR, :]
+            col = (n - ROTATED_GROUPS) * GROUP
+            bias = v_bias[:, col : col + GROUP]
+            if by_gpsimd:
+                copied = work.tile([P, GROUP], F32, tag="copied", bufs=2)
+                nc.scalar.copy(out=copied[:], in_=acc[:])
+                nc.gpsimd.tensor_tensor(out=row, in0=copied[:], in1=bias, op=ADD)
+            else:
+                nc.vector.tensor_tensor(out=row, in0=acc[:], in1=bias, op=ADD)
 
         def flip_back(n, c, pair):
             summed = psum_plain.tile([P, PAIR, HALF_GROUP], F32, tag="plain")
             bare = psum_plain.tile([P, PAIR, HALF_GROUP], F32, tag="plain")
             banks[n, c, pair] = (summed, bare)
-            result = work.tile([P, PAIR, GROUP], F32, tag="result", bufs=8)
-            results[n, c, pair] = result
-            for jj in range(PAIR):
-                block = slice((pair * PAIR + jj) * P, (pair * PAIR + jj + 1) * P)
+            new_result(n, c, pair)
+            blocks = [slice(b * P, (b + 1) * P) for b in range(pair * PAIR, (pair + 1) * PAIR)]
+            for j, block in enumerate(blocks):
+                for m in range(TILES):
+                    nc.tensor.transpose(
+                        out=bare[:, j, m * P : (m + 1) * P],
+                        in_=products[n, c, TILES + m][:, block],
+                        identity=ident[:],
+                    )
+            for j, block in enumerate(blocks):
                 for m in range(TILES):
                     for i, order in enumerate((ident, swap)):
                         nc.tensor.matmul(
-                            out=summed[:, jj, m * P : (m + 1) * P],
+                            out=summed[:, j, m * P : (m + 1) * P],
                             lhsT=products[n, c, m][:, i, block],
                             rhs=order[:],
                             is_transpose=True,
                             start=(i == 0),
                             stop=(i == 1),
                         )
-            for jj in range(PAIR):
-                block = slice((pair * PAIR + jj) * P, (pair * PAIR + jj + 1) * P)
-                for m in range(TILES):
-                    nc.tensor.transpose(
-                        out=bare[:, jj, m * P : (m + 1) * P], in_=products[n, c, TILES + m][:, block], identity=ident[:]
-                    )
 
-        def finish_summed(n, c, pair):
+        def finish_rotated(n, c, pair, ready, cos_on_gpsimd):
             summed, bare = banks[n, c, pair]
-            nc.scalar.copy(out=results[n, c, pair][:, :, 0:HALF_GROUP], in_=summed[:])
-
-        def finish_bare(n, c, pair, between):
-            summed, bare = banks[n, c, pair]
+            result = results[n, c, pair]
             blocks = slice(c * CHUNK_BLOCKS + pair * PAIR, c * CHUNK_BLOCKS + (pair + 1) * PAIR)
             heads = HALF_GROUP // DH
             by_cos = work.tile([P, PAIR, HALF_GROUP], F32, tag="by_cos", bufs=2)
             by_sin = work.tile([P, PAIR, HALF_GROUP], F32, tag="by_sin", bufs=2)
-            nc.vector.tensor_tensor(
+            if cos_on_gpsimd:
+                copied = work.tile([P, GROUP], F32, tag="copied", bufs=2)
+                nc.scalar.copy(out=copied[:], in_=bare[:].rearrange("p b n -> p (b n)"))
+                engine, source = nc.gpsimd, copied[:].rearrange("p (b h d) -> p b h d", b=PAIR, d=DH)
+            else:
+                engine, source = nc.vector, bare[:].rearrange("p b (h d) -> p b h d", d=DH)
+            engine.tensor_tensor(
                 out=by_cos[:].rearrange("p b (h d) -> p b h d", d=DH),
-                in0=bare[:].rearrange("p b (h d) -> p b h d", d=DH),
+                in0=source,
                 in1=cos_raw[:, blocks, :].unsqueeze(2).to_broadcast([P, PAIR, heads, DH]),
                 op=MULT,
             )
-            if between:
-                quantise_weights(*between)
+            if ready:
+                quantise_weights(*ready)
             nc.vector.tensor_tensor(
                 out=by_sin[:].rearrange("p b (h i two) -> p b h i two", h=heads, two=2),
                 in0=bare[:].rearrange("p b (h i two) -> p b h i two", h=heads, two=2)[:, :, :, :, ::-1],
-                in1=sin_signed[:, blocks, :].rearrange("p b (i two) -> p b i two", two=2).unsqueeze(2).to_broadcast([P, PAIR, heads, HALF, 2]),
+                in1=sin_signed[:, blocks, :]
+                .rearrange("p b (i two) -> p b i two", two=2)
+                .unsqueeze(2)
+                .to_broadcast([P, PAIR, heads, HALF, 2]),
                 op=MULT,
             )
+            nc.scalar.copy(out=result[:, :, 0:HALF_GROUP], in_=summed[:])
             nc.gpsimd.tensor_tensor(
-                out=results[n, c, pair][:, :, HALF_GROUP:GROUP], in0=by_cos[:], in1=by_sin[:], op=ADD
+                out=result[:, :, HALF_GROUP:GROUP], in0=by_cos[:], in1=by_sin[:], op=ADD
             )
-
-        def emit_plain(n, c, m):
-            acc = accs[n, c, m]
-            pair = m // PAIR
-            if m % PAIR == 0:
-                result = work.tile([P, PAIR, GROUP], F32, tag="result", bufs=8)
-                results[n, c, pair] = result
-            row = results[n, c, pair][:, m % PAIR, :]
-            col = (n - ROTATED_GROUPS) * GROUP
-            nc.vector.tensor_tensor(out=row, in0=acc[:], in1=v_bias[:, col : col + GROUP], op=ADD)
-            if m % PAIR == PAIR - 1:
-                store(n, c, pair)
+            store(n, c, pair)
 
         def multiply_pair(n, c, pair):
-            for m in (2 * pair, 2 * pair + 1):
+            for m in range(pair * PAIR, (pair + 1) * PAIR):
                 multiply(n, c, m)
 
-        def emit_pair(n, c, pair):
-            for m in (2 * pair, 2 * pair + 1):
-                emit_plain(n, c, m)
+        def leave_pair(n, c, pair, by_gpsimd):
+            for m in range(pair * PAIR, (pair + 1) * PAIR):
+                leave_plain(n, c, m, m in by_gpsimd)
+            store(n, c, pair)
 
-        group_weights(first, 0, "V", 0, 1)
-        flip_positions(0, "S")
-        flip_positions(1, "S")
-        quantise_weights(first, 0)
-        group_weights(first, 1, "V", 0, 1)
+        group_weights("vector", v_first, 0, 0, GROUP)
+        flip_positions(0)
+        quantise_weights(v_first, 0)
+        group_weights("vector", v_first, 1, 0, GROUP)
         quantise_positions(0)
-        quantise_weights(first, 1)
+        quantise_weights(v_first, 1)
         spread_v_bias()
         flip_bias()
-        flip_positions(2, "S")
-        flip_positions(3, "S")
-        multiply_pair(first, 0, 0)
+        flip_positions(1)
+        multiply_pair(v_first, 0, 0)
         spread_tables()
         quantise_positions(1)
-        emit_pair(first, 0, 0)
-        flip_positions(4, "S")
-        flip_positions(5, "S")
-        multiply_pair(first, 0, 1)
+        leave_pair(v_first, 0, 0, ())
+        flip_positions(2)
+        multiply_pair(v_first, 0, 1)
         quantise_positions(2)
-        emit_pair(first, 0, 1)
-        flip_positions(6, "S")
-        flip_positions(7, "S")
-        group_weights(second, 1, "S", 0, 2)
-        group_weights(second, 1, "S", 1, 2)
-        multiply_pair(first, 1, 0)
-        group_weights(second, 0, "G", 0, 4)
-        group_weights(second, 0, "G", 1, 4)
+        leave_pair(v_first, 0, 1, ())
+        flip_positions(3)
+        for part in range(2):
+            group_weights("scalar", 0, 1, part * GROUP // 2, (part + 1) * GROUP // 2)
+        multiply_pair(v_first, 1, 0)
+        for part in range(2):
+            group_weights("gpsimd", 0, 0, part * GROUP // 4, (part + 1) * GROUP // 4)
         quantise_positions(3)
-        group_weights(second, 0, "G", 2, 4)
-        group_weights(second, 0, "G", 3, 4)
-        emit_pair(first, 1, 0)
+        for part in range(2, 4):
+            group_weights("gpsimd", 0, 0, part * GROUP // 4, (part + 1) * GROUP // 4)
+        leave_pair(v_first, 1, 0, ())
         flip_tables(0)
-        quantise_weights(second, 0)
-        multiply_pair(first, 1, 1)
-        quantise_weights(second, 1)
-        emit_pair(first, 1, 1)
+        quantise_weights(0, 0)
+        multiply_pair(v_first, 1, 1)
+        quantise_weights(0, 1)
+        leave_pair(v_first, 1, 1, ())
         flip_tables(1)
-        group_weights(1, 0, "S", 0, 2)
-        group_weights(1, 0, "S", 1, 2)
-        for h, step in enumerate(HALVES):
-            kind, n, c, pair = step
-            before = (n, c - 1) if c else (n - 1, 1)
-            rotated = kind == "R"
-            mine = (pair, TILES + pair) if rotated else (2 * pair, 2 * pair + 1)
-            finishing = None
-            if kind == "F":
-                finishing = (n, c)
-            elif kind == "R" and before[0] >= 0:
-                finishing = before
-            if kind != "F":
-                for m in mine:
+        pieces = [(n, g) for n in list(range(1, ROTATED_GROUPS)) + [v_last] for g in range(PASSES)]
+        parts = [(n, g, part) for n, g in pieces for part in range(2)]
+        units = [(n, c) for n in range(ROTATED_GROUPS) for c in range(CHUNKS)]
+        LEAD = 2
+
+        def regroup(index):
+            if index < len(parts):
+                n, g, part = parts[index]
+                group_weights("scalar", n, g, part * GROUP // 2, (part + 1) * GROUP // 2)
+
+        def ready_piece(h):
+            return pieces[h // 2] if h % 2 == 0 and h // 2 < len(pieces) else None
+
+        for index in range(LEAD):
+            regroup(index)
+        previous = None
+        for u, (n, c) in enumerate(units):
+            for pair in range(PAIRS):
+                h = u * PAIRS + pair
+                for m in (pair, TILES + pair):
                     multiply(n, c, m)
-            if finishing:
-                flip_back(*finishing, pair)
-            if kind != "F":
-                for m in mine:
-                    emit_transposed(n, c, m) if rotated else emit_plain(n, c, m)
-            ready = QUANTISE.get(h)
-            if finishing:
-                finish_summed(*finishing, pair)
-                finish_bare(*finishing, pair, ready)
-                store(*finishing, pair)
-            elif ready:
-                quantise_weights(*ready)
-            for n2, g2, engine, part, parts in REGROUP.get(h, ()):
-                group_weights(n2, g2, engine, part, parts)
+                if previous:
+                    flip_back(*previous, pair)
+                for m in (pair, TILES + pair):
+                    leave_rotated(n, c, m)
+                ready = ready_piece(h)
+                if previous:
+                    finish_rotated(*previous, pair, ready, (u, pair) in ())
+                elif ready:
+                    quantise_weights(*ready)
+                regroup(h + LEAD)
+            previous = (n, c)
+        for c in range(CHUNKS):
+            for pair in range(PAIRS):
+                multiply_pair(v_last, c, pair)
+                if c == 0:
+                    flip_back(*previous, pair)
+                leave_pair(v_last, c, pair, ())
+                if c == 0:
+                    finish_rotated(*previous, pair, ready_piece(len(units) * PAIRS + pair), (len(units), pair) in ())

@@ -121,7 +121,7 @@ def tile_arlowvisionattention_pa_kernel(
         nc.sync.dma_start(out=sin_raw[:], in_=sin.rearrange("(p b) d -> p b d", b=S_BLOCKS))
         load_positions(2)
         load_positions(3)
-        for n in list(range(ROTATED_GROUPS)) + [v_last]:
+        for n in [0, 1, 2, v_last, 3]:
             for g in range(PASSES):
                 load_weights(n, g)
 
@@ -304,7 +304,7 @@ def tile_arlowvisionattention_pa_kernel(
             col = (n - ROTATED_GROUPS) * GROUP
             bias = v_bias[:, col : col + GROUP]
             if by_gpsimd:
-                copied = work.tile([P, GROUP], F32, tag="copied", bufs=2)
+                copied = work.tile([P, GROUP], F32, tag="copied", bufs=3)
                 nc.scalar.copy(out=copied[:], in_=acc[:])
                 nc.gpsimd.tensor_tensor(out=row, in0=copied[:], in1=bias, op=ADD)
             else:
@@ -335,22 +335,16 @@ def tile_arlowvisionattention_pa_kernel(
                             stop=(i == 1),
                         )
 
-        def finish_rotated(n, c, pair, ready, cos_on_gpsimd):
+        def finish_rotated(n, c, pair, ready, adder):
             summed, bare = banks[n, c, pair]
             result = results[n, c, pair]
             blocks = slice(c * CHUNK_BLOCKS + pair * PAIR, c * CHUNK_BLOCKS + (pair + 1) * PAIR)
             heads = HALF_GROUP // DH
-            by_cos = work.tile([P, PAIR, HALF_GROUP], F32, tag="by_cos", bufs=2)
-            by_sin = work.tile([P, PAIR, HALF_GROUP], F32, tag="by_sin", bufs=2)
-            if cos_on_gpsimd:
-                copied = work.tile([P, GROUP], F32, tag="copied", bufs=2)
-                nc.scalar.copy(out=copied[:], in_=bare[:].rearrange("p b n -> p (b n)"))
-                engine, source = nc.gpsimd, copied[:].rearrange("p (b h d) -> p b h d", b=PAIR, d=DH)
-            else:
-                engine, source = nc.vector, bare[:].rearrange("p b (h d) -> p b h d", d=DH)
-            engine.tensor_tensor(
+            by_cos = work.tile([P, PAIR, HALF_GROUP], F32, tag="by_cos", bufs=3)
+            by_sin = work.tile([P, PAIR, HALF_GROUP], F32, tag="by_sin", bufs=3)
+            nc.vector.tensor_tensor(
                 out=by_cos[:].rearrange("p b (h d) -> p b h d", d=DH),
-                in0=source,
+                in0=bare[:].rearrange("p b (h d) -> p b h d", d=DH),
                 in1=cos_raw[:, blocks, :].unsqueeze(2).to_broadcast([P, PAIR, heads, DH]),
                 op=MULT,
             )
@@ -366,7 +360,7 @@ def tile_arlowvisionattention_pa_kernel(
                 op=MULT,
             )
             nc.scalar.copy(out=result[:, :, 0:HALF_GROUP], in_=summed[:])
-            nc.gpsimd.tensor_tensor(
+            adder.tensor_tensor(
                 out=result[:, :, HALF_GROUP:GROUP], in0=by_cos[:], in1=by_sin[:], op=ADD
             )
             store(n, c, pair)
@@ -401,11 +395,11 @@ def tile_arlowvisionattention_pa_kernel(
         for part in range(2):
             group_weights("scalar", 0, 1, part * GROUP // 2, (part + 1) * GROUP // 2)
         multiply_pair(v_first, 1, 0)
-        for part in range(2):
-            group_weights("gpsimd", 0, 0, part * GROUP // 4, (part + 1) * GROUP // 4)
+        for part in range(4):
+            group_weights("gpsimd", 0, 0, part * GROUP // 8, (part + 1) * GROUP // 8)
         quantise_positions(3)
-        for part in range(2, 4):
-            group_weights("gpsimd", 0, 0, part * GROUP // 4, (part + 1) * GROUP // 4)
+        for part in range(4, 8):
+            group_weights("gpsimd", 0, 0, part * GROUP // 8, (part + 1) * GROUP // 8)
         leave_pair(v_first, 1, 0, ())
         flip_tables(0)
         quantise_weights(0, 0)
@@ -413,9 +407,10 @@ def tile_arlowvisionattention_pa_kernel(
         quantise_weights(0, 1)
         leave_pair(v_first, 1, 1, ())
         flip_tables(1)
-        pieces = [(n, g) for n in list(range(1, ROTATED_GROUPS)) + [v_last] for g in range(PASSES)]
+        order = [0, 1, 2, v_last, 3]
+        pieces = [(n, g) for n in order[1:] for g in range(PASSES)]
         parts = [(n, g, part) for n, g in pieces for part in range(2)]
-        units = [(n, c) for n in range(ROTATED_GROUPS) for c in range(CHUNKS)]
+        units = [(n, c) for n in order for c in range(CHUNKS)]
         LEAD = 2
 
         def regroup(index):
@@ -424,32 +419,36 @@ def tile_arlowvisionattention_pa_kernel(
                 group_weights("scalar", n, g, part * GROUP // 2, (part + 1) * GROUP // 2)
 
         def ready_piece(h):
+            if h <= 1:
+                return pieces[0] if h == 1 else None
             return pieces[h // 2] if h % 2 == 0 and h // 2 < len(pieces) else None
 
         for index in range(LEAD):
             regroup(index)
         previous = None
         for u, (n, c) in enumerate(units):
+            rotated = n < ROTATED_GROUPS
             for pair in range(PAIRS):
                 h = u * PAIRS + pair
-                for m in (pair, TILES + pair):
+                ready = ready_piece(h)
+                mine = (pair, TILES + pair) if rotated else (pair * PAIR, pair * PAIR + 1)
+                for m in mine:
                     multiply(n, c, m)
                 if previous:
                     flip_back(*previous, pair)
-                for m in (pair, TILES + pair):
-                    leave_rotated(n, c, m)
-                ready = ready_piece(h)
+                if rotated:
+                    for m in mine:
+                        leave_rotated(n, c, m)
+                else:
+                    if ready and not previous:
+                        quantise_weights(*ready)
+                    leave_pair(n, c, pair, (0, 2))
                 if previous:
-                    finish_rotated(*previous, pair, ready, (u, pair) in ())
-                elif ready:
+                    finish_rotated(*previous, pair, ready, nc.gpsimd)
+                elif ready and rotated:
                     quantise_weights(*ready)
                 regroup(h + LEAD)
-            previous = (n, c)
-        for c in range(CHUNKS):
-            for pair in range(PAIRS):
-                multiply_pair(v_last, c, pair)
-                if c == 0:
-                    flip_back(*previous, pair)
-                leave_pair(v_last, c, pair, ())
-                if c == 0:
-                    finish_rotated(*previous, pair, ready_piece(len(units) * PAIRS + pair), (len(units), pair) in ())
+            previous = (n, c) if rotated else None
+        for pair in range(PAIRS):
+            flip_back(*previous, pair)
+            finish_rotated(*previous, pair, None, (nc.gpsimd, nc.vector)[pair])

@@ -402,29 +402,33 @@ def tile_arlowvisionattention_pa_kernel(
             group_weights("gpsimd", 0, 0, part * GROUP // 8, (part + 1) * GROUP // 8)
         leave_pair(v_first, 1, 0, ())
         flip_tables(0)
+        group_weights("scalar", 1, 0, 0, GROUP // 2)
         quantise_weights(0, 0)
         multiply_pair(v_first, 1, 1)
         quantise_weights(0, 1)
         leave_pair(v_first, 1, 1, ())
         flip_tables(1)
+        group_weights("scalar", 1, 0, GROUP // 2, GROUP)
         order = [0, 1, 2, v_last, 3]
         pieces = [(n, g) for n in order[1:] for g in range(PASSES)]
         parts = [(n, g, part) for n, g in pieces for part in range(2)]
         units = [(n, c) for n in order for c in range(CHUNKS)]
         LEAD = 2
 
+        def shared(i):
+            return 1 < i <= 6
+
         def regroup(index):
             if index < len(parts):
                 n, g, part = parts[index]
-                group_weights("scalar", n, g, part * GROUP // 2, (part + 1) * GROUP // 2)
+                width = 384 if shared(index // 2) else GROUP
+                group_weights("scalar", n, g, part * width // 2, (part + 1) * width // 2)
 
         def ready_piece(h):
             if h <= 1:
                 return pieces[0] if h == 1 else None
             return pieces[h // 2] if h % 2 == 0 and h // 2 < len(pieces) else None
 
-        for index in range(LEAD):
-            regroup(index)
         previous = None
         for u, (n, c) in enumerate(units):
             rotated = n < ROTATED_GROUPS
@@ -448,6 +452,8 @@ def tile_arlowvisionattention_pa_kernel(
                 elif ready and rotated:
                     quantise_weights(*ready)
                 regroup(h + LEAD)
+                if h % 2 == 0 and h // 2 + 1 < len(pieces) and shared(h // 2 + 1):
+                    group_weights("gpsimd", *pieces[h // 2 + 1], 384, GROUP)
             previous = (n, c) if rotated else None
         for pair in range(PAIRS):
             flip_back(*previous, pair)

@@ -199,7 +199,10 @@ def tile_arlowvisionattention_pa_kernel(
                     in_=raw.rearrange("q t (c i) -> q c t i", i=4),
                 )
             elif engine == "vector":
-                nc.vector.tensor_copy(out=out, in_=raw.rearrange("q t c -> q c t"))
+                nc.vector.tensor_copy(
+                    out=out.rearrange("q (c i) t -> q c t i", i=4),
+                    in_=raw.rearrange("q t (c i) -> q c t i", i=4),
+                )
             else:
                 nc.gpsimd.tensor_scalar(
                     out=out, in0=raw.rearrange("q t c -> q c t"),
@@ -451,7 +454,10 @@ def tile_arlowvisionattention_pa_kernel(
                     finish_rotated(*previous, pair, ready, nc.gpsimd)
                 elif ready and rotated:
                     quantise_weights(*ready)
-                regroup(h + LEAD)
+                if h == 1:
+                    regroup(LEAD)
+                if h > 0:
+                    regroup(h + LEAD)
                 if h % 2 == 0 and h // 2 + 1 < len(pieces) and shared(h // 2 + 1):
                     group_weights("gpsimd", *pieces[h // 2 + 1], 384, GROUP)
             previous = (n, c) if rotated else None

@@ -195,13 +195,13 @@ def tile_arlowvisionattention_pa_kernel(
             raw = w_raw[n][:, g, :, first:last]
             if engine == "scalar":
                 nc.scalar.copy(
-                    out=out.rearrange("q (c i) t -> q c t i", i=4),
-                    in_=raw.rearrange("q t (c i) -> q c t i", i=4),
+                    out=out.rearrange("q (c i) t -> q c t i", i=8),
+                    in_=raw.rearrange("q t (c i) -> q c t i", i=8),
                 )
             elif engine == "vector":
                 nc.vector.tensor_copy(
-                    out=out.rearrange("q (c i) t -> q c t i", i=4),
-                    in_=raw.rearrange("q t (c i) -> q c t i", i=4),
+                    out=out.rearrange("q (c i) t -> q c t i", i=8),
+                    in_=raw.rearrange("q t (c i) -> q c t i", i=8),
                 )
             else:
                 nc.gpsimd.tensor_scalar(
@@ -391,26 +391,26 @@ def tile_arlowvisionattention_pa_kernel(
         quantise_positions(1)
         leave_pair(v_first, 0, 0, ())
         flip_positions(2)
+        flip_positions(3)
         multiply_pair(v_first, 0, 1)
         quantise_positions(2)
         leave_pair(v_first, 0, 1, ())
-        flip_positions(3)
         for part in range(2):
             group_weights("scalar", 0, 1, part * GROUP // 2, (part + 1) * GROUP // 2)
         multiply_pair(v_first, 1, 0)
         for part in range(4):
             group_weights("gpsimd", 0, 0, part * GROUP // 8, (part + 1) * GROUP // 8)
-        quantise_positions(3)
         for part in range(4, 8):
             group_weights("gpsimd", 0, 0, part * GROUP // 8, (part + 1) * GROUP // 8)
         leave_pair(v_first, 1, 0, ())
+        quantise_positions(3)
         flip_tables(0)
+        flip_tables(1)
         group_weights("scalar", 1, 0, 0, GROUP // 2)
         quantise_weights(0, 0)
         multiply_pair(v_first, 1, 1)
         quantise_weights(0, 1)
         leave_pair(v_first, 1, 1, ())
-        flip_tables(1)
         group_weights("scalar", 1, 0, GROUP // 2, GROUP)
         order = [0, 1, 2, v_last, 3]
         pieces = [(n, g) for n in order[1:] for g in range(PASSES)]

@@ -23,15 +23,20 @@ S_BLOCKS = S // P
 CHUNK_BLOCKS = 4
 CHUNK = CHUNK_BLOCKS * P
 CHUNKS = S_BLOCKS // CHUNK_BLOCKS
+PAIR = 2
+PAIRS = CHUNK_BLOCKS // PAIR
 GROUP = 512
 GROUPS = 3 * WIDTH // GROUP
 ROTATED_GROUPS = 2 * WIDTH // GROUP
 GROUP_TILES = GROUP // P
 TILES = GROUP_TILES // 2
-HALF_GROUP = TILES * P
+SIDE = TILES * P
 TILE_HEADS = P // DH
-PAIR = 2
-PAIRS = CHUNK_BLOCKS // PAIR
+BIAS_ROWS = 3 * WIDTH // P
+ROTATED_ROWS = 2 * WIDTH // P
+RUN = 4
+SCALAR_COLUMNS = 3 * GROUP // 4
+GPSIMD_COLUMNS = 64
 
 FLOPS = 2 * S * E * 3 * WIDTH
 
@@ -52,10 +57,11 @@ def tile_arlowvisionattention_pa_kernel(
             out.rearrange("(p b) h d -> p b (h d)", b=S_BLOCKS) for out in (out_0, out_1, out_2)
         ]
 
-        x_raw = [operands.tile([P, PAIR, E], BF16, name="x_raw%d" % i) for i in range(S_BLOCKS // PAIR)]
+        pair_indices = range(S_BLOCKS // PAIR)
+        x_raw = [operands.tile([P, PAIR, E], BF16, name="x_raw%d" % i) for i in pair_indices]
         x_grouped = [
             operands.tile([P, PASSES, PAIR * P, PACK], BF16, name="x_grouped%d" % i, align_bytes=64)
-            for i in range(S_BLOCKS // PAIR)
+            for i in pair_indices
         ]
         x_codes = [
             operands.tile([P, PASSES, CHUNK], U32, name="x_codes%d" % c, align_bytes=64)
@@ -79,9 +85,8 @@ def tile_arlowvisionattention_pa_kernel(
         cos_raw = const.tile([P, S_BLOCKS, DH], BF16)
         sin_raw = const.tile([P, S_BLOCKS, DH], BF16)
         sin_signed = const.tile([P, S_BLOCKS, DH], BF16)
-        rotated_tiles = ROTATED_GROUPS * GROUP_TILES
         bias_rows = const.tile([P, P], BF16)
-        bias_cols = const.tile([P, rotated_tiles], F32)
+        bias_cols = const.tile([P, ROTATED_ROWS], F32)
         v_bias = const.tile([P, WIDTH], F32)
         ident = const.tile([P, P], F32)
         ident_bf16 = const.tile([P, P], BF16)
@@ -91,29 +96,30 @@ def tile_arlowvisionattention_pa_kernel(
         spread_sin = const.tile([P, S_BLOCKS, TILE_HEADS, DH], BF16)
         table_t = const.tile([P, 2, CHUNKS * CHUNK], BF16)
 
-        schedule = tc.manual_schedule()
-        ctx.enter_context(schedule)
+        ctx.enter_context(tc.manual_schedule())
+
+        nc.gpsimd.memset(bias_rows[:], 0.0)
+        nc.gpsimd.memset(warm[:], 0.0)
+        make_identity(nc, ident[:])
+        nc.scalar.copy(out=warm[:, 1:2], in_=warm[:, 0:1])
 
         def load_weights(n, g):
             nc.sync.dma_start(
                 out=w_raw[n][:, g, :, :],
                 in_=w_qkv[
                     g * K_PASS : (g + 1) * K_PASS, n * GROUP : (n + 1) * GROUP
-                ].rearrange("(q t) n -> q t n", t=PACK),
+                ].rearrange("(p t) n -> p t n", t=PACK),
             )
 
         def load_positions(i):
             nc.sync.dma_start(out=x_raw[i][:], in_=x_rows[:, i * PAIR : (i + 1) * PAIR, :])
 
-        v_first, v_last = ROTATED_GROUPS, ROTATED_GROUPS + 1
-        nc.gpsimd.memset(bias_rows[:], 0.0)
-        nc.gpsimd.memset(warm[:], 0.0)
-        make_identity(nc, ident[:])
-        nc.scalar.copy(out=warm[:, 1:2], in_=warm[:, 0:1])
+        v_first, v_last = range(ROTATED_GROUPS, GROUPS)
+        later_groups = [0, 1, 2, v_last, 3]
         load_weights(v_first, 0)
         load_positions(0)
         nc.sync.dma_start(
-            out=bias_rows[0 : 3 * WIDTH // P, :], in_=b_qkv.rearrange("(t n) -> t n", n=P)
+            out=bias_rows[0:BIAS_ROWS, :], in_=b_qkv.rearrange("(r n) -> r n", n=P)
         )
         load_weights(v_first, 1)
         load_positions(1)
@@ -121,7 +127,7 @@ def tile_arlowvisionattention_pa_kernel(
         nc.sync.dma_start(out=sin_raw[:], in_=sin.rearrange("(p b) d -> p b d", b=S_BLOCKS))
         load_positions(2)
         load_positions(3)
-        for n in [0, 1, 2, v_last, 3]:
+        for n in later_groups:
             for g in range(PASSES):
                 load_weights(n, g)
 
@@ -141,7 +147,9 @@ def tile_arlowvisionattention_pa_kernel(
                 )
                 nc.vector.tensor_scalar_mul(
                     out=spread_pairs[:, :, :, :, 1 - two],
-                    in0=sin_pairs[:, :, :, two].unsqueeze(2).to_broadcast([P, S_BLOCKS, TILE_HEADS, HALF]),
+                    in0=sin_pairs[:, :, :, two]
+                    .unsqueeze(2)
+                    .to_broadcast([P, S_BLOCKS, TILE_HEADS, HALF]),
                     scalar1=sign,
                 )
             nc.vector.tensor_copy(
@@ -166,13 +174,13 @@ def tile_arlowvisionattention_pa_kernel(
         def flip_bias():
             flipped = psum_plain.tile([P, P], BF16, tag="plain")
             nc.tensor.transpose(out=flipped[:], in_=bias_rows[:], identity=ident_bf16[:])
-            nc.vector.tensor_copy(out=bias_cols[:], in_=flipped[:, 0:rotated_tiles])
+            nc.vector.tensor_copy(out=bias_cols[:], in_=flipped[:, 0:ROTATED_ROWS])
 
         def spread_v_bias():
             for n in range(WIDTH // GROUP):
                 spread = psum_plain.tile([P, GROUP_TILES, P], F32, tag="plain")
                 for m in range(GROUP_TILES):
-                    row = rotated_tiles + n * GROUP_TILES + m
+                    row = ROTATED_ROWS + n * GROUP_TILES + m
                     nc.tensor.matmul(
                         out=spread[:, m, :],
                         lhsT=ident_bf16[:, row : row + 1].to_broadcast([P, P]),
@@ -187,33 +195,33 @@ def tile_arlowvisionattention_pa_kernel(
 
         grouped = {}
 
-        def group_weights(engine, n, g, first, last):
+        def regroup(engine, n, g, first, last):
             if first == 0:
                 w_grouped = work.tile([P, GROUP, PACK], BF16, align_bytes=64, tag="w_grouped", bufs=4)
                 grouped[n, g] = w_grouped
             out = grouped[n, g][:, first:last, :]
             raw = w_raw[n][:, g, :, first:last]
-            if engine == "scalar":
-                nc.scalar.copy(
-                    out=out.rearrange("q (c i) t -> q c t i", i=8),
-                    in_=raw.rearrange("q t (c i) -> q c t i", i=8),
-                )
-            elif engine == "vector":
-                nc.vector.tensor_copy(
-                    out=out.rearrange("q (c i) t -> q c t i", i=8),
-                    in_=raw.rearrange("q t (c i) -> q c t i", i=8),
+            if engine == "gpsimd":
+                nc.gpsimd.tensor_scalar(
+                    out=out,
+                    in0=raw.rearrange("p t c -> p c t"),
+                    scalar1=1.0,
+                    scalar2=0.0,
+                    op0=MULT,
+                    op1=ADD,
                 )
             else:
-                nc.gpsimd.tensor_scalar(
-                    out=out, in0=raw.rearrange("q t c -> q c t"),
-                    scalar1=1.0, scalar2=0.0, op0=MULT, op1=ADD,
+                copy = nc.scalar.copy if engine == "scalar" else nc.vector.tensor_copy
+                copy(
+                    out=out.rearrange("p (c i) t -> p c t i", i=RUN),
+                    in_=raw.rearrange("p t (c i) -> p c t i", i=RUN),
                 )
 
         def quantise_weights(n, g):
             nc.vector.quantize_mx(
                 out=w_codes[n][:, g, :].bitcast(FP8X4),
                 scales=w_scales[n][:, g, :],
-                in_=grouped[n, g][:].rearrange("q c t -> q (c t)"),
+                in_=grouped[n, g][:].rearrange("p c t -> p (c t)"),
             )
 
         def flip_positions(i):
@@ -229,7 +237,7 @@ def tile_arlowvisionattention_pa_kernel(
                         )
                 nc.scalar.copy(
                     out=x_grouped[i][:].bitcast(F32)[:, :, j * P : (j + 1) * P, :],
-                    in_=flipped[:].rearrange("q g u s -> q g s u"),
+                    in_=flipped[:].rearrange("p g u s -> p g s u"),
                 )
 
         def quantise_positions(i):
@@ -238,25 +246,10 @@ def tile_arlowvisionattention_pa_kernel(
                 nc.vector.quantize_mx(
                     out=x_codes[c][:, g, col : col + PAIR * P].bitcast(FP8X4),
                     scales=x_scales[c][:, g, col : col + PAIR * P],
-                    in_=x_grouped[i][:, g, :, :].rearrange("q s t -> q (s t)"),
+                    in_=x_grouped[i][:, g, :, :].rearrange("p s t -> p (s t)"),
                 )
 
-        results = {}
-        accs = {}
-        products = {}
-        banks = {}
-
-        def new_result(n, c, pair):
-            result = work.tile([P, PAIR, GROUP], F32, tag="result", bufs=8)
-            results[n, c, pair] = result
-
-        def store(n, c, pair):
-            which, col = divmod(n * GROUP, WIDTH)
-            first_block = c * CHUNK_BLOCKS + pair * PAIR
-            nc.sync.dma_start(
-                out=out_rows[which][:, first_block : first_block + PAIR, col : col + GROUP],
-                in_=results[n, c, pair][:],
-            )
+        accs, products, banks, results = {}, {}, {}, {}
 
         def multiply(n, c, m):
             acc = psum_mx.tile([P, GROUP], F32, tag="acc")
@@ -278,6 +271,18 @@ def tile_arlowvisionattention_pa_kernel(
                     stop=(g == PASSES - 1),
                 )
 
+        def new_result(n, c, pair):
+            result = work.tile([P, PAIR, GROUP], F32, tag="result", bufs=8)
+            results[n, c, pair] = result
+
+        def store(n, c, pair):
+            which, col = divmod(n * GROUP, WIDTH)
+            first_block = c * CHUNK_BLOCKS + pair * PAIR
+            nc.sync.dma_start(
+                out=out_rows[which][:, first_block : first_block + PAIR, col : col + GROUP],
+                in_=results[n, c, pair][:],
+            )
+
         def leave_rotated(n, c, m):
             acc = accs[n, c, m]
             tile_index = n * GROUP_TILES + m
@@ -298,26 +303,25 @@ def tile_arlowvisionattention_pa_kernel(
                 nc.scalar.activation(out=biased[:], in_=acc[:], func=IDENTITY, bias=bias, scale=1.0)
                 products[n, c, m] = biased
 
-        def leave_plain(n, c, m, by_gpsimd):
-            acc = accs[n, c, m]
-            pair = m // PAIR
-            if m % PAIR == 0:
-                new_result(n, c, pair)
-            row = results[n, c, pair][:, m % PAIR, :]
+        def leave_plain(n, c, pair, by_gpsimd):
+            new_result(n, c, pair)
             col = (n - ROTATED_GROUPS) * GROUP
             bias = v_bias[:, col : col + GROUP]
-            if by_gpsimd:
-                copied = work.tile([P, GROUP], F32, tag="copied", bufs=3)
-                nc.scalar.copy(out=copied[:], in_=acc[:])
-                nc.gpsimd.tensor_tensor(out=row, in0=copied[:], in1=bias, op=ADD)
-            else:
-                nc.vector.tensor_tensor(out=row, in0=acc[:], in1=bias, op=ADD)
+            for j in range(PAIR):
+                acc = accs[n, c, pair * PAIR + j]
+                row = results[n, c, pair][:, j, :]
+                if j < by_gpsimd:
+                    copied = work.tile([P, GROUP], F32, tag="copied", bufs=3)
+                    nc.scalar.copy(out=copied[:], in_=acc[:])
+                    nc.gpsimd.tensor_tensor(out=row, in0=copied[:], in1=bias, op=ADD)
+                else:
+                    nc.vector.tensor_tensor(out=row, in0=acc[:], in1=bias, op=ADD)
+            store(n, c, pair)
 
         def flip_back(n, c, pair):
-            summed = psum_plain.tile([P, PAIR, HALF_GROUP], F32, tag="plain")
-            bare = psum_plain.tile([P, PAIR, HALF_GROUP], F32, tag="plain")
+            summed = psum_plain.tile([P, PAIR, SIDE], F32, tag="plain")
+            bare = psum_plain.tile([P, PAIR, SIDE], F32, tag="plain")
             banks[n, c, pair] = (summed, bare)
-            new_result(n, c, pair)
             blocks = [slice(b * P, (b + 1) * P) for b in range(pair * PAIR, (pair + 1) * PAIR)]
             for j, block in enumerate(blocks):
                 for m in range(TILES):
@@ -340,11 +344,13 @@ def tile_arlowvisionattention_pa_kernel(
 
         def finish_rotated(n, c, pair, ready, adder):
             summed, bare = banks[n, c, pair]
+            new_result(n, c, pair)
             result = results[n, c, pair]
-            blocks = slice(c * CHUNK_BLOCKS + pair * PAIR, c * CHUNK_BLOCKS + (pair + 1) * PAIR)
-            heads = HALF_GROUP // DH
-            by_cos = work.tile([P, PAIR, HALF_GROUP], F32, tag="by_cos", bufs=3)
-            by_sin = work.tile([P, PAIR, HALF_GROUP], F32, tag="by_sin", bufs=3)
+            first_block = c * CHUNK_BLOCKS + pair * PAIR
+            blocks = slice(first_block, first_block + PAIR)
+            heads = SIDE // DH
+            by_cos = work.tile([P, PAIR, SIDE], F32, tag="by_cos", bufs=3)
+            by_sin = work.tile([P, PAIR, SIDE], F32, tag="by_sin", bufs=3)
             nc.vector.tensor_tensor(
                 out=by_cos[:].rearrange("p b (h d) -> p b h d", d=DH),
                 in0=bare[:].rearrange("p b (h d) -> p b h d", d=DH),
@@ -362,105 +368,81 @@ def tile_arlowvisionattention_pa_kernel(
                 .to_broadcast([P, PAIR, heads, HALF, 2]),
                 op=MULT,
             )
-            nc.scalar.copy(out=result[:, :, 0:HALF_GROUP], in_=summed[:])
-            adder.tensor_tensor(
-                out=result[:, :, HALF_GROUP:GROUP], in0=by_cos[:], in1=by_sin[:], op=ADD
-            )
+            nc.scalar.copy(out=result[:, :, 0:SIDE], in_=summed[:])
+            adder.tensor_tensor(out=result[:, :, SIDE:GROUP], in0=by_cos[:], in1=by_sin[:], op=ADD)
             store(n, c, pair)
 
-        def multiply_pair(n, c, pair):
+        def multiply_plain(n, c, pair):
             for m in range(pair * PAIR, (pair + 1) * PAIR):
                 multiply(n, c, m)
 
-        def leave_pair(n, c, pair, by_gpsimd):
-            for m in range(pair * PAIR, (pair + 1) * PAIR):
-                leave_plain(n, c, m, m in by_gpsimd)
-            store(n, c, pair)
+        def regroup_on_gpsimd(n, g, first, last):
+            for col in range(first, last, GPSIMD_COLUMNS):
+                regroup("gpsimd", n, g, col, col + GPSIMD_COLUMNS)
 
-        group_weights("vector", v_first, 0, 0, GROUP)
+        regroup("vector", v_first, 0, 0, GROUP)
         flip_positions(0)
         quantise_weights(v_first, 0)
-        group_weights("vector", v_first, 1, 0, GROUP)
+        regroup("vector", v_first, 1, 0, GROUP)
         quantise_positions(0)
         quantise_weights(v_first, 1)
         spread_v_bias()
         flip_bias()
         flip_positions(1)
-        multiply_pair(v_first, 0, 0)
+        multiply_plain(v_first, 0, 0)
         spread_tables()
         quantise_positions(1)
-        leave_pair(v_first, 0, 0, ())
+        leave_plain(v_first, 0, 0, by_gpsimd=0)
         flip_positions(2)
         flip_positions(3)
-        multiply_pair(v_first, 0, 1)
+        multiply_plain(v_first, 0, 1)
         quantise_positions(2)
-        leave_pair(v_first, 0, 1, ())
-        for part in range(2):
-            group_weights("scalar", 0, 1, part * GROUP // 2, (part + 1) * GROUP // 2)
-        multiply_pair(v_first, 1, 0)
-        for part in range(4):
-            group_weights("gpsimd", 0, 0, part * GROUP // 8, (part + 1) * GROUP // 8)
-        for part in range(4, 8):
-            group_weights("gpsimd", 0, 0, part * GROUP // 8, (part + 1) * GROUP // 8)
-        leave_pair(v_first, 1, 0, ())
+        leave_plain(v_first, 0, 1, by_gpsimd=0)
+        for first in (0, GROUP // 2):
+            regroup("scalar", 0, 1, first, first + GROUP // 2)
+        multiply_plain(v_first, 1, 0)
+        regroup_on_gpsimd(0, 0, 0, GROUP)
+        leave_plain(v_first, 1, 0, by_gpsimd=0)
         quantise_positions(3)
-        flip_tables(0)
-        flip_tables(1)
-        group_weights("scalar", 1, 0, 0, GROUP // 2)
+        for c in range(CHUNKS):
+            flip_tables(c)
+        regroup("scalar", 1, 0, 0, GROUP // 2)
         quantise_weights(0, 0)
-        multiply_pair(v_first, 1, 1)
+        multiply_plain(v_first, 1, 1)
         quantise_weights(0, 1)
-        leave_pair(v_first, 1, 1, ())
-        group_weights("scalar", 1, 0, GROUP // 2, GROUP)
-        order = [0, 1, 2, v_last, 3]
-        pieces = [(n, g) for n in order[1:] for g in range(PASSES)]
-        parts = [(n, g, part) for n, g in pieces for part in range(2)]
-        units = [(n, c) for n in order for c in range(CHUNKS)]
-        LEAD = 2
+        leave_plain(v_first, 1, 1, by_gpsimd=0)
+        regroup("scalar", 1, 0, GROUP // 2, GROUP)
 
-        def shared(i):
-            return 1 < i <= 6
-
-        def regroup(index):
-            if index < len(parts):
-                n, g, part = parts[index]
-                width = 384 if shared(index // 2) else GROUP
-                group_weights("scalar", n, g, part * width // 2, (part + 1) * width // 2)
-
-        def ready_piece(h):
-            if h <= 1:
-                return pieces[0] if h == 1 else None
-            return pieces[h // 2] if h % 2 == 0 and h // 2 < len(pieces) else None
-
+        pieces = [(n, g) for n in later_groups[1:] for g in range(PASSES)]
+        units = [(n, c) for n in later_groups for c in range(CHUNKS)]
         previous = None
         for u, (n, c) in enumerate(units):
             rotated = n < ROTATED_GROUPS
+            shared = rotated and previous is not None
             for pair in range(PAIRS):
-                h = u * PAIRS + pair
-                ready = ready_piece(h)
-                mine = (pair, TILES + pair) if rotated else (pair * PAIR, pair * PAIR + 1)
-                for m in mine:
+                quantising = u < len(pieces) and pair == (1 if u == 0 else 0)
+                ready = pieces[u] if quantising else None
+                tiles = (pair, TILES + pair) if rotated else (pair * PAIR, pair * PAIR + 1)
+                for m in tiles:
                     multiply(n, c, m)
                 if previous:
                     flip_back(*previous, pair)
+                if ready and not previous:
+                    quantise_weights(*ready)
                 if rotated:
-                    for m in mine:
+                    for m in tiles:
                         leave_rotated(n, c, m)
                 else:
-                    if ready and not previous:
-                        quantise_weights(*ready)
-                    leave_pair(n, c, pair, (0, 2))
+                    leave_plain(n, c, pair, by_gpsimd=1)
                 if previous:
                     finish_rotated(*previous, pair, ready, nc.gpsimd)
-                elif ready and rotated:
-                    quantise_weights(*ready)
-                if h == 1:
-                    regroup(LEAD)
-                if h > 0:
-                    regroup(h + LEAD)
-                if h % 2 == 0 and h // 2 + 1 < len(pieces) and shared(h // 2 + 1):
-                    group_weights("gpsimd", *pieces[h // 2 + 1], 384, GROUP)
+                if u + 1 < len(pieces):
+                    columns = SCALAR_COLUMNS if shared else GROUP
+                    part = columns // PAIRS
+                    regroup("scalar", *pieces[u + 1], pair * part, (pair + 1) * part)
+                    if shared and pair == 0:
+                        regroup("gpsimd", *pieces[u + 1], columns, GROUP)
             previous = (n, c) if rotated else None
-        for pair in range(PAIRS):
+        for pair, adder in enumerate((nc.gpsimd, nc.vector)):
             flip_back(*previous, pair)
-            finish_rotated(*previous, pair, None, (nc.gpsimd, nc.vector)[pair])
+            finish_rotated(*previous, pair, None, adder)

@@ -82,18 +82,17 @@ def tile_arlowvisionattention_pa_kernel(
             operands.tile([P, PASSES, GROUP], U8, name="w_scales%d" % n, align_bytes=64)
             for n in range(GROUPS)
         ]
-        cos_raw = const.tile([P, S_BLOCKS, DH], BF16)
         sin_raw = const.tile([P, S_BLOCKS, DH], BF16)
-        sin_signed = const.tile([P, S_BLOCKS, DH], BF16)
+        cos_raw = const.tile([P, S_BLOCKS, DH], BF16)
+        factors = const.tile([P, S_BLOCKS, 2, DH], BF16)
         bias_rows = const.tile([P, P], BF16)
         bias_cols = const.tile([P, ROTATED_ROWS], F32)
-        v_bias = const.tile([P, WIDTH], F32)
+        v_bias = const.tile([P, WIDTH], BF16)
         ident = const.tile([P, P], F32)
         ident_bf16 = const.tile([P, P], BF16)
         swap = const.tile([P, P], F32)
         warm = const.tile([P, 2], F32)
-        spread_cos = const.tile([P, S_BLOCKS, TILE_HEADS, DH], BF16)
-        spread_sin = const.tile([P, S_BLOCKS, TILE_HEADS, DH], BF16)
+        spread = const.tile([P, 2, S_BLOCKS, TILE_HEADS, DH], BF16)
         table_t = const.tile([P, 2, CHUNKS * CHUNK], BF16)
 
         ctx.enter_context(tc.manual_schedule())
@@ -139,31 +138,28 @@ def tile_arlowvisionattention_pa_kernel(
 
         def spread_tables():
             sin_pairs = sin_raw[:].rearrange("p b (i two) -> p b i two", two=2)
-            signed_pairs = sin_signed[:].rearrange("p b (i two) -> p b i two", two=2)
-            spread_pairs = spread_sin[:].rearrange("p b h (i two) -> p b h i two", two=2)
+            factor_pairs = factors[:, :, 1, :].rearrange("p b (i two) -> p b i two", two=2)
+
+            def scaled_copy(out, in_, by):
+                nc.gpsimd.tensor_scalar(out=out, in0=in_, scalar1=by, scalar2=0.0, op0=MULT, op1=ADD)
+
             for two, sign in ((0, -1.0), (1, 1.0)):
-                nc.vector.tensor_scalar_mul(
-                    out=signed_pairs[:, :, :, two], in0=sin_pairs[:, :, :, two], scalar1=sign
+                scaled_copy(factor_pairs[:, :, :, 1 - two], sin_pairs[:, :, :, two], sign)
+            for which, table in ((1, factors[:, :, 1, :]), (0, cos_raw[:])):
+                scaled_copy(
+                    spread[:, which, :, :, :],
+                    table.unsqueeze(2).to_broadcast([P, S_BLOCKS, TILE_HEADS, DH]),
+                    1.0,
                 )
-                nc.vector.tensor_scalar_mul(
-                    out=spread_pairs[:, :, :, :, 1 - two],
-                    in0=sin_pairs[:, :, :, two]
-                    .unsqueeze(2)
-                    .to_broadcast([P, S_BLOCKS, TILE_HEADS, HALF]),
-                    scalar1=sign,
-                )
-            nc.vector.tensor_copy(
-                out=spread_cos[:],
-                in_=cos_raw[:].unsqueeze(2).to_broadcast([P, S_BLOCKS, TILE_HEADS, DH]),
-            )
+            scaled_copy(factors[:, :, 0, :], cos_raw[:], 1.0)
 
         def flip_tables(c):
-            for i, table in enumerate((spread_cos, spread_sin)):
+            for i in range(2):
                 flipped = psum_plain.tile([P, CHUNK_BLOCKS, P], BF16, tag="plain")
                 for j in range(CHUNK_BLOCKS):
                     nc.tensor.transpose(
                         out=flipped[:, j, :],
-                        in_=table[:, c * CHUNK_BLOCKS + j, :, :].rearrange("p h d -> p (h d)"),
+                        in_=spread[:, i, c * CHUNK_BLOCKS + j, :, :].rearrange("p h d -> p (h d)"),
                         identity=ident_bf16[:],
                     )
                 nc.scalar.copy(
@@ -177,21 +173,17 @@ def tile_arlowvisionattention_pa_kernel(
             nc.vector.tensor_copy(out=bias_cols[:], in_=flipped[:, 0:ROTATED_ROWS])
 
         def spread_v_bias():
-            for n in range(WIDTH // GROUP):
-                spread = psum_plain.tile([P, GROUP_TILES, P], F32, tag="plain")
-                for m in range(GROUP_TILES):
-                    row = ROTATED_ROWS + n * GROUP_TILES + m
-                    nc.tensor.matmul(
-                        out=spread[:, m, :],
-                        lhsT=ident_bf16[:, row : row + 1].to_broadcast([P, P]),
-                        rhs=bias_rows[:],
-                        start=True,
-                        stop=True,
-                    )
-                nc.scalar.copy(
-                    out=v_bias[:, n * GROUP : (n + 1) * GROUP],
-                    in_=spread[:].rearrange("p m n -> p (m n)"),
+            rows = psum_plain.tile([P, WIDTH // P, P], BF16, tag="plain")
+            for m in range(WIDTH // P):
+                row = ROTATED_ROWS + m
+                nc.tensor.matmul(
+                    out=rows[:, m, :],
+                    lhsT=ident_bf16[:, row : row + 1].to_broadcast([P, P]),
+                    rhs=bias_rows[:],
+                    start=True,
+                    stop=True,
                 )
+            nc.scalar.copy(out=v_bias[:], in_=rows[:].rearrange("p m n -> p (m n)"))
 
         grouped = {}
 
@@ -349,27 +341,25 @@ def tile_arlowvisionattention_pa_kernel(
             first_block = c * CHUNK_BLOCKS + pair * PAIR
             blocks = slice(first_block, first_block + PAIR)
             heads = SIDE // DH
-            by_cos = work.tile([P, PAIR, SIDE], F32, tag="by_cos", bufs=3)
-            by_sin = work.tile([P, PAIR, SIDE], F32, tag="by_sin", bufs=3)
-            nc.vector.tensor_tensor(
-                out=by_cos[:].rearrange("p b (h d) -> p b h d", d=DH),
-                in0=bare[:].rearrange("p b (h d) -> p b h d", d=DH),
-                in1=cos_raw[:, blocks, :].unsqueeze(2).to_broadcast([P, PAIR, heads, DH]),
-                op=MULT,
-            )
+            by = work.tile([P, PAIR, 2, SIDE], F32, tag="by", bufs=3)
             if ready:
                 quantise_weights(*ready)
             nc.vector.tensor_tensor(
-                out=by_sin[:].rearrange("p b (h i two) -> p b h i two", h=heads, two=2),
-                in0=bare[:].rearrange("p b (h i two) -> p b h i two", h=heads, two=2)[:, :, :, :, ::-1],
-                in1=sin_signed[:, blocks, :]
-                .rearrange("p b (i two) -> p b i two", two=2)
+                out=by[:].rearrange("p b w (h d) -> p b w h d", d=DH),
+                in0=bare[:]
+                .rearrange("p b (h d) -> p b h d", d=DH)
                 .unsqueeze(2)
-                .to_broadcast([P, PAIR, heads, HALF, 2]),
+                .to_broadcast([P, PAIR, 2, heads, DH]),
+                in1=factors[:, blocks, :, :].unsqueeze(3).to_broadcast([P, PAIR, 2, heads, DH]),
                 op=MULT,
             )
             nc.scalar.copy(out=result[:, :, 0:SIDE], in_=summed[:])
-            adder.tensor_tensor(out=result[:, :, SIDE:GROUP], in0=by_cos[:], in1=by_sin[:], op=ADD)
+            adder.tensor_tensor(
+                out=result[:, :, SIDE:GROUP].rearrange("p b (i two) -> p b i two", two=2),
+                in0=by[:, :, 0, :].rearrange("p b (i two) -> p b i two", two=2),
+                in1=by[:, :, 1, :].rearrange("p b (i two) -> p b i two", two=2)[:, :, :, ::-1],
+                op=ADD,
+            )
             store(n, c, pair)
 
         def multiply_plain(n, c, pair):

@@ -129,6 +129,10 @@ def tile_arlowvisionattention_pa_kernel(
         for n in later_groups:
             for g in range(PASSES):
                 load_weights(n, g)
+            if n == later_groups[0]:
+                nc.sync.dma_start(
+                    out=factors[:, :, 0, :], in_=cos.rearrange("(p b) d -> p b d", b=S_BLOCKS)
+                )
 
         swap_pairs = swap[:].rearrange("r (i two) -> r i two", two=2)
         ident_pairs = ident[:].rearrange("r (i two) -> r i two", two=2)
@@ -140,18 +144,15 @@ def tile_arlowvisionattention_pa_kernel(
             sin_pairs = sin_raw[:].rearrange("p b (i two) -> p b i two", two=2)
             factor_pairs = factors[:, :, 1, :].rearrange("p b (i two) -> p b i two", two=2)
 
-            def scaled_copy(out, in_, by):
-                nc.gpsimd.tensor_scalar(out=out, in0=in_, scalar1=by, scalar2=0.0, op0=MULT, op1=ADD)
-
             for two, sign in ((0, -1.0), (1, 1.0)):
-                scaled_copy(factor_pairs[:, :, :, 1 - two], sin_pairs[:, :, :, two], sign)
-            for which, table in ((1, factors[:, :, 1, :]), (0, cos_raw[:])):
-                scaled_copy(
-                    spread[:, which, :, :, :],
-                    table.unsqueeze(2).to_broadcast([P, S_BLOCKS, TILE_HEADS, DH]),
-                    1.0,
+                nc.vector.tensor_scalar_mul(
+                    out=factor_pairs[:, :, :, 1 - two], in0=sin_pairs[:, :, :, two], scalar1=sign
                 )
-            scaled_copy(factors[:, :, 0, :], cos_raw[:], 1.0)
+            for which, table in ((1, factors[:, :, 1, :]), (0, cos_raw[:])):
+                nc.vector.tensor_copy(
+                    out=spread[:, which, :, :, :],
+                    in_=table.unsqueeze(2).to_broadcast([P, S_BLOCKS, TILE_HEADS, DH]),
+                )
 
         def flip_tables(c):
             for i in range(2):

@@ -343,8 +343,6 @@ def tile_arlowvisionattention_pa_kernel(
             blocks = slice(first_block, first_block + PAIR)
             heads = SIDE // DH
             by = work.tile([P, PAIR, 2, SIDE], F32, tag="by", bufs=3)
-            if ready:
-                quantise_weights(*ready)
             nc.vector.tensor_tensor(
                 out=by[:].rearrange("p b w (h d) -> p b w h d", d=DH),
                 in0=bare[:]
@@ -354,6 +352,8 @@ def tile_arlowvisionattention_pa_kernel(
                 in1=factors[:, blocks, :, :].unsqueeze(3).to_broadcast([P, PAIR, 2, heads, DH]),
                 op=MULT,
             )
+            if ready:
+                quantise_weights(*ready)
             nc.scalar.copy(out=result[:, :, 0:SIDE], in_=summed[:])
             adder.tensor_tensor(
                 out=result[:, :, SIDE:GROUP].rearrange("p b (i two) -> p b i two", two=2),

from contextlib import ExitStack

import concourse.mybir as mybir
from concourse.masks import make_identity

F32 = mybir.dt.float32
BF16 = mybir.dt.bfloat16
U32 = mybir.dt.uint32
U8 = mybir.dt.uint8
FP8X4 = mybir.dt.float8_e4m3fn_x4
ADD = mybir.AluOpType.add
MULT = mybir.AluOpType.mult
IDENTITY = mybir.ActivationFunctionType.Identity

S, E, HEADS, DH = 1024, 1024, 16, 64
WIDTH = HEADS * DH
HALF = DH // 2
P = 128
PACK = 4
K_PASS = P * PACK
PASSES = E // K_PASS
S_BLOCKS = S // P
CHUNK_BLOCKS = 4
CHUNK = CHUNK_BLOCKS * P
CHUNKS = S_BLOCKS // CHUNK_BLOCKS
PAIR = 2
PAIRS = CHUNK_BLOCKS // PAIR
GROUP = 512
GROUPS = 3 * WIDTH // GROUP
ROTATED_GROUPS = 2 * WIDTH // GROUP
GROUP_TILES = GROUP // P
TILES = GROUP_TILES // 2
SIDE = TILES * P
TILE_HEADS = P // DH
BIAS_ROWS = 3 * WIDTH // P
ROTATED_ROWS = 2 * WIDTH // P
RUN = 4
SCALAR_COLUMNS = 3 * GROUP // 4
GPSIMD_COLUMNS = 64

FLOPS = 2 * S * E * 3 * WIDTH


def tile_arlowvisionattention_pa_kernel(
    tc, hidden_states, cos, sin, w_qkv, b_qkv, out_0, out_1, out_2
):
    nc = tc.nc
    with ExitStack() as ctx:
        const = ctx.enter_context(tc.tile_pool(name="const", bufs=1))
        operands = ctx.enter_context(tc.tile_pool(name="operands", bufs=1))
        work = ctx.enter_context(tc.tile_pool(name="work", bufs=3))
        psum_mx = ctx.enter_context(tc.psum_pool(name="psum_mx", bufs=4))
        psum_plain = ctx.enter_context(tc.psum_pool(name="psum_plain", bufs=4))

        x_rows = hidden_states.rearrange("(p b) k -> p b k", b=S_BLOCKS)
        out_rows = [
            out.rearrange("(p b) h d -> p b (h d)", b=S_BLOCKS) for out in (out_0, out_1, out_2)
        ]

        pair_indices = range(S_BLOCKS // PAIR)
        x_raw = [operands.tile([P, PAIR, E], BF16, name="x_raw%d" % i) for i in pair_indices]
        x_grouped = [
            operands.tile([P, PASSES, PAIR * P, PACK], BF16, name="x_grouped%d" % i, align_bytes=64)
            for i in pair_indices
        ]
        x_codes = [
            operands.tile([P, PASSES, CHUNK], U32, name="x_codes%d" % c, align_bytes=64)
            for c in range(CHUNKS)
        ]
        x_scales = [
            operands.tile([P, PASSES, CHUNK], U8, name="x_scales%d" % c, align_bytes=64)
            for c in range(CHUNKS)
        ]
        w_raw = [
            operands.tile([P, PASSES, PACK, GROUP], BF16, name="w_raw%d" % n) for n in range(GROUPS)
        ]
        w_codes = [
            operands.tile([P, PASSES, GROUP], U32, name="w_codes%d" % n, align_bytes=64)
            for n in range(GROUPS)
        ]
        w_scales = [
            operands.tile([P, PASSES, GROUP], U8, name="w_scales%d" % n, align_bytes=64)
            for n in range(GROUPS)
        ]
        sin_raw = const.tile([P, S_BLOCKS, DH], BF16)
        cos_raw = const.tile([P, S_BLOCKS, DH], BF16)
        factors = const.tile([P, S_BLOCKS, 2, DH], BF16)
        bias_rows = const.tile([P, P], BF16)
        bias_cols = const.tile([P, ROTATED_ROWS], F32)
        v_bias = const.tile([P, WIDTH], BF16)
        ident = const.tile([P, P], F32)
        ident_bf16 = const.tile([P, P], BF16)
        swap = const.tile([P, P], F32)
        warm = const.tile([P, 2], F32)
        spread = const.tile([P, 2, S_BLOCKS, TILE_HEADS, DH], BF16)
        table_t = const.tile([P, 2, CHUNKS * CHUNK], BF16)

        ctx.enter_context(tc.manual_schedule())

        nc.gpsimd.memset(bias_rows[:], 0.0)
        nc.gpsimd.memset(warm[:], 0.0)
        make_identity(nc, ident[:])
        nc.scalar.copy(out=warm[:, 1:2], in_=warm[:, 0:1])

        def load_weights(n, g):
            nc.sync.dma_start(
                out=w_raw[n][:, g, :, :],
                in_=w_qkv[
                    g * K_PASS : (g + 1) * K_PASS, n * GROUP : (n + 1) * GROUP
                ].rearrange("(p t) n -> p t n", t=PACK),
            )

        def load_positions(i):
            nc.sync.dma_start(out=x_raw[i][:], in_=x_rows[:, i * PAIR : (i + 1) * PAIR, :])

        v_first, v_last = range(ROTATED_GROUPS, GROUPS)
        later_groups = [0, 1, 2, v_last, 3]
        load_weights(v_first, 0)
        load_positions(0)
        nc.sync.dma_start(
            out=bias_rows[0:BIAS_ROWS, :], in_=b_qkv.rearrange("(r n) -> r n", n=P)
        )
        load_weights(v_first, 1)
        load_positions(1)
        nc.sync.dma_start(out=cos_raw[:], in_=cos.rearrange("(p b) d -> p b d", b=S_BLOCKS))
        nc.sync.dma_start(out=sin_raw[:], in_=sin.rearrange("(p b) d -> p b d", b=S_BLOCKS))
        load_positions(2)
        load_positions(3)
        for n in later_groups:
            for g in range(PASSES):
                load_weights(n, g)
            if n == later_groups[0]:
                nc.sync.dma_start(
                    out=factors[:, :, 0, :], in_=cos.rearrange("(p b) d -> p b d", b=S_BLOCKS)
                )

        swap_pairs = swap[:].rearrange("r (i two) -> r i two", two=2)
        ident_pairs = ident[:].rearrange("r (i two) -> r i two", two=2)
        nc.vector.tensor_copy(out=ident_bf16[:], in_=ident[:])
        for two in range(2):
            nc.vector.tensor_copy(out=swap_pairs[:, :, two], in_=ident_pairs[:, :, 1 - two])

        def spread_tables():
            sin_pairs = sin_raw[:].rearrange("p b (i two) -> p b i two", two=2)
            factor_pairs = factors[:, :, 1, :].rearrange("p b (i two) -> p b i two", two=2)

            for two, sign in ((0, -1.0), (1, 1.0)):
                nc.vector.tensor_scalar_mul(
                    out=factor_pairs[:, :, :, 1 - two], in0=sin_pairs[:, :, :, two], scalar1=sign
                )
            for which, table in ((1, factors[:, :, 1, :]), (0, cos_raw[:])):
                nc.vector.tensor_copy(
                    out=spread[:, which, :, :, :],
                    in_=table.unsqueeze(2).to_broadcast([P, S_BLOCKS, TILE_HEADS, DH]),
                )

        def flip_tables(c):
            for i in range(2):
                flipped = psum_plain.tile([P, CHUNK_BLOCKS, P], BF16, tag="plain")
                for j in range(CHUNK_BLOCKS):
                    nc.tensor.transpose(
                        out=flipped[:, j, :],
                        in_=spread[:, i, c * CHUNK_BLOCKS + j, :, :].rearrange("p h d -> p (h d)"),
                        identity=ident_bf16[:],
                    )
                nc.scalar.copy(
                    out=table_t[:, i, c * CHUNK : (c + 1) * CHUNK],
                    in_=flipped[:].rearrange("r j p -> r (j p)"),
                )

        def flip_bias():
            flipped = psum_plain.tile([P, P], BF16, tag="plain")
            nc.tensor.transpose(out=flipped[:], in_=bias_rows[:], identity=ident_bf16[:])
            nc.vector.tensor_copy(out=bias_cols[:], in_=flipped[:, 0:ROTATED_ROWS])

        def spread_v_bias():
            rows = psum_plain.tile([P, WIDTH // P, P], BF16, tag="plain")
            for m in range(WIDTH // P):
                row = ROTATED_ROWS + m
                nc.tensor.matmul(
                    out=rows[:, m, :],
                    lhsT=ident_bf16[:, row : row + 1].to_broadcast([P, P]),
                    rhs=bias_rows[:],
                    start=True,
                    stop=True,
                )
            nc.scalar.copy(out=v_bias[:], in_=rows[:].rearrange("p m n -> p (m n)"))

        grouped = {}

        def regroup(engine, n, g, first, last):
            if first == 0:
                w_grouped = work.tile([P, GROUP, PACK], BF16, align_bytes=64, tag="w_grouped", bufs=4)
                grouped[n, g] = w_grouped
            out = grouped[n, g][:, first:last, :]
            raw = w_raw[n][:, g, :, first:last]
            if engine == "gpsimd":
                nc.gpsimd.tensor_scalar(
                    out=out,
                    in0=raw.rearrange("p t c -> p c t"),
                    scalar1=1.0,
                    scalar2=0.0,
                    op0=MULT,
                    op1=ADD,
                )
            else:
                copy = nc.scalar.copy if engine == "scalar" else nc.vector.tensor_copy
                copy(
                    out=out.rearrange("p (c i) t -> p c t i", i=RUN),
                    in_=raw.rearrange("p t (c i) -> p c t i", i=RUN),
                )

        def quantise_weights(n, g):
            nc.vector.quantize_mx(
                out=w_codes[n][:, g, :].bitcast(FP8X4),
                scales=w_scales[n][:, g, :],
                in_=grouped[n, g][:].rearrange("p c t -> p (c t)"),
            )

        def flip_positions(i):
            for j in range(PAIR):
                words = x_raw[i][:, j, :].bitcast(F32)
                flipped = psum_plain.tile([P, PASSES, 2, P], F32, tag="plain")
                for g in range(PASSES):
                    for u in range(2):
                        nc.tensor.transpose(
                            out=flipped[:, g, u, :],
                            in_=words[:, g * 2 * P + u : (g + 1) * 2 * P : 2],
                            identity=ident[:],
                        )
                nc.scalar.copy(
                    out=x_grouped[i][:].bitcast(F32)[:, :, j * P : (j + 1) * P, :],
                    in_=flipped[:].rearrange("p g u s -> p g s u"),
                )

        def quantise_positions(i):
            c, col = divmod(i * PAIR * P, CHUNK)
            for g in range(PASSES):
                nc.vector.quantize_mx(
                    out=x_codes[c][:, g, col : col + PAIR * P].bitcast(FP8X4),
                    scales=x_scales[c][:, g, col : col + PAIR * P],
                    in_=x_grouped[i][:, g, :, :].rearrange("p s t -> p (s t)"),
                )

        accs, products, banks, results = {}, {}, {}, {}

        def multiply(n, c, m):
            acc = psum_mx.tile([P, GROUP], F32, tag="acc")
            accs[n, c, m] = acc
            mine, everything = slice(m * P, (m + 1) * P), slice(0, GROUP)
            weights, positions = (w_codes[n], w_scales[n]), (x_codes[c], x_scales[c])
            if n < ROTATED_GROUPS:
                stationary, moving = weights, positions
            else:
                stationary, moving = positions, weights
            for g in range(PASSES):
                nc.tensor.matmul_mx(
                    out=acc[:],
                    lhsT=stationary[0][:, g, mine].bitcast(FP8X4),
                    lhsT_scale=stationary[1][:, g, mine],
                    rhs=moving[0][:, g, everything].bitcast(FP8X4),
                    rhs_scale=moving[1][:, g, everything],
                    start=(g == 0),
                    stop=(g == PASSES - 1),
                )

        def new_result(n, c, pair):
            result = work.tile([P, PAIR, GROUP], F32, tag="result", bufs=8)
            results[n, c, pair] = result

        def store(n, c, pair):
            which, col = divmod(n * GROUP, WIDTH)
            first_block = c * CHUNK_BLOCKS + pair * PAIR
            nc.sync.dma_start(
                out=out_rows[which][:, first_block : first_block + PAIR, col : col + GROUP],
                in_=results[n, c, pair][:],
            )

        def leave_rotated(n, c, m):
            acc = accs[n, c, m]
            tile_index = n * GROUP_TILES + m
            bias = bias_cols[:, tile_index : tile_index + 1]
            if m < TILES:
                both = work.tile([P, 2, CHUNK], F32, tag="both", bufs=2 * TILES + 1)
                nc.vector.scalar_tensor_tensor(
                    out=both[:],
                    in0=acc[:].unsqueeze(1).to_broadcast([P, 2, CHUNK]),
                    scalar=bias,
                    in1=table_t[:, :, c * CHUNK : (c + 1) * CHUNK],
                    op0=ADD,
                    op1=MULT,
                )
                products[n, c, m] = both
            else:
                biased = work.tile([P, CHUNK], F32, tag="biased", bufs=2 * TILES + 1)
                nc.scalar.activation(out=biased[:], in_=acc[:], func=IDENTITY, bias=bias, scale=1.0)
                products[n, c, m] = biased

        def leave_plain(n, c, pair, by_gpsimd):
            new_result(n, c, pair)
            col = (n - ROTATED_GROUPS) * GROUP
            bias = v_bias[:, col : col + GROUP]
            for j in range(PAIR):
                acc = accs[n, c, pair * PAIR + j]
                row = results[n, c, pair][:, j, :]
                if j < by_gpsimd:
                    copied = work.tile([P, GROUP], F32, tag="copied", bufs=3)
                    nc.scalar.copy(out=copied[:], in_=acc[:])
                    nc.gpsimd.tensor_tensor(out=row, in0=copied[:], in1=bias, op=ADD)
                else:
                    nc.vector.tensor_tensor(out=row, in0=acc[:], in1=bias, op=ADD)
            store(n, c, pair)

        def flip_back(n, c, pair):
            summed = psum_plain.tile([P, PAIR, SIDE], F32, tag="plain")
            bare = psum_plain.tile([P, PAIR, SIDE], F32, tag="plain")
            banks[n, c, pair] = (summed, bare)
            blocks = [slice(b * P, (b + 1) * P) for b in range(pair * PAIR, (pair + 1) * PAIR)]
            for j, block in enumerate(blocks):
                for m in range(TILES):
                    nc.tensor.transpose(
                        out=bare[:, j, m * P : (m + 1) * P],
                        in_=products[n, c, TILES + m][:, block],
                        identity=ident[:],
                    )
            for j, block in enumerate(blocks):
                for m in range(TILES):
                    for i, order in enumerate((ident, swap)):
                        nc.tensor.matmul(
                            out=summed[:, j, m * P : (m + 1) * P],
                            lhsT=products[n, c, m][:, i, block],
                            rhs=order[:],
                            is_transpose=True,
                            start=(i == 0),
                            stop=(i == 1),
                        )

        def finish_rotated(n, c, pair, ready, adder):
            summed, bare = banks[n, c, pair]
            new_result(n, c, pair)
            result = results[n, c, pair]
            first_block = c * CHUNK_BLOCKS + pair * PAIR
            blocks = slice(first_block, first_block + PAIR)
            heads = SIDE // DH
            by = work.tile([P, PAIR, 2, SIDE], F32, tag="by", bufs=3)
            nc.vector.tensor_tensor(
                out=by[:].rearrange("p b w (h d) -> p b w h d", d=DH),
                in0=bare[:]
                .rearrange("p b (h d) -> p b h d", d=DH)
                .unsqueeze(2)
                .to_broadcast([P, PAIR, 2, heads, DH]),
                in1=factors[:, blocks, :, :].unsqueeze(3).to_broadcast([P, PAIR, 2, heads, DH]),
                op=MULT,
            )
            if ready:
                quantise_weights(*ready)
            nc.scalar.copy(out=result[:, :, 0:SIDE], in_=summed[:])
            adder.tensor_tensor(
                out=result[:, :, SIDE:GROUP].rearrange("p b (i two) -> p b i two", two=2),
                in0=by[:, :, 0, :].rearrange("p b (i two) -> p b i two", two=2),
                in1=by[:, :, 1, :].rearrange("p b (i two) -> p b i two", two=2)[:, :, :, ::-1],
                op=ADD,
            )
            store(n, c, pair)

        def multiply_plain(n, c, pair):
            for m in range(pair * PAIR, (pair + 1) * PAIR):
                multiply(n, c, m)

        def regroup_on_gpsimd(n, g, first, last):
            for col in range(first, last, GPSIMD_COLUMNS):
                regroup("gpsimd", n, g, col, col + GPSIMD_COLUMNS)

        regroup("vector", v_first, 0, 0, GROUP)
        flip_positions(0)
        quantise_weights(v_first, 0)
        regroup("vector", v_first, 1, 0, GROUP)
        quantise_positions(0)
        quantise_weights(v_first, 1)
        spread_v_bias()
        flip_bias()
        flip_positions(1)
        multiply_plain(v_first, 0, 0)
        spread_tables()
        quantise_positions(1)
        leave_plain(v_first, 0, 0, by_gpsimd=0)
        flip_positions(2)
        flip_positions(3)
        multiply_plain(v_first, 0, 1)
        quantise_positions(2)
        leave_plain(v_first, 0, 1, by_gpsimd=0)
        for first in (0, GROUP // 2):
            regroup("scalar", 0, 1, first, first + GROUP // 2)
        multiply_plain(v_first, 1, 0)
        regroup_on_gpsimd(0, 0, 0, GROUP)
        leave_plain(v_first, 1, 0, by_gpsimd=0)
        quantise_positions(3)
        for c in range(CHUNKS):
            flip_tables(c)
        regroup("scalar", 1, 0, 0, GROUP // 2)
        quantise_weights(0, 0)
        multiply_plain(v_first, 1, 1)
        quantise_weights(0, 1)
        leave_plain(v_first, 1, 1, by_gpsimd=0)
        regroup("scalar", 1, 0, GROUP // 2, GROUP)

        pieces = [(n, g) for n in later_groups[1:] for g in range(PASSES)]
        units = [(n, c) for n in later_groups for c in range(CHUNKS)]
        previous = None
        for u, (n, c) in enumerate(units):
            rotated = n < ROTATED_GROUPS
            shared = rotated and previous is not None
            for pair in range(PAIRS):
                quantising = u < len(pieces) and pair == (1 if u == 0 else 0)
                ready = pieces[u] if quantising else None
                tiles = (pair, TILES + pair) if rotated else (pair * PAIR, pair * PAIR + 1)
                for m in tiles:
                    multiply(n, c, m)
                if previous:
                    flip_back(*previous, pair)
                if ready and not previous:
                    quantise_weights(*ready)
                if rotated:
                    for m in tiles:
                        leave_rotated(n, c, m)
                else:
                    leave_plain(n, c, pair, by_gpsimd=1)
                if previous:
                    finish_rotated(*previous, pair, ready, nc.gpsimd)
                if u + 1 < len(pieces):
                    columns = SCALAR_COLUMNS if shared else GROUP
                    part = columns // PAIRS
                    regroup("scalar", *pieces[u + 1], pair * part, (pair + 1) * part)
                    if shared and pair == 0:
                        regroup("gpsimd", *pieces[u + 1], columns, GROUP)
            previous = (n, c) if rotated else None
        for pair, adder in enumerate((nc.gpsimd, nc.vector)):
            flip_back(*previous, pair)
            finish_rotated(*previous, pair, None, adder)
